import numpy as np
import ml_dtypes


def mxq(x, axis, fmt="e4m3"):
    dtype, down = {"e4m3": (ml_dtypes.float8_e4m3fn, 7), "e5m2": (ml_dtypes.float8_e5m2, 14)}[fmt]
    v = np.moveaxis(np.asarray(x, np.float32).astype(ml_dtypes.bfloat16).astype(np.float64), axis, -1)
    blocks = v.reshape(v.shape[:-1] + (-1, 32))
    amax = np.abs(blocks).max(-1, keepdims=True)
    byte = np.maximum(np.where(amax > 0, np.frexp(amax)[1] - 1 + 127, 0) - down, 1)
    scale = np.exp2(byte - 127.0)
    codes = (blocks / scale).astype(np.float32).astype(dtype).astype(np.float64)
    return np.moveaxis((codes * scale).reshape(v.shape), -1, axis)


WIDE = False


def mx_kscale(k):
    if not WIDE:
        return np.ones(k)
    levels = np.array([10, -10, 5, -5, 0])
    a = np.random.permutation(np.resize(levels, k // 512 * 4)).reshape(k // 512, 4)
    idx = np.arange(k)
    return np.exp2(a[idx // 512, idx % 128 // 32])


BF16 = ml_dtypes.bfloat16


def bf(x):
    return np.asarray(x, np.float32).astype(BF16)


def f64(x):
    return np.asarray(x).astype(np.float64)


E2M1 = np.array([0.0, 0.5, 1.0, 1.5, 2.0, 3.0, 4.0, 6.0, -0.0, -0.5, -1.0, -1.5, -2.0, -3.0, -4.0, -6.0])


def pack_weight(w, fmt):
    k, n = w.shape
    w = f64(bf(w)).reshape(k // 32, 32, n)
    amax = np.abs(w).max(1)
    if fmt == "e4m3":
        byte = np.frexp(amax)[1] - 1 + 127 - 7
    else:
        mant, ex = np.frexp(amax / 6.0)
        byte = np.where(mant > 0.5, ex, ex - 1) + 127
    byte = np.clip(np.where(amax > 0, byte, 1), 1, 254)
    scaled = (w * np.exp2(127.0 - byte)[:, None, :]).reshape(k, n).astype(np.float32)
    by_word = np.ascontiguousarray(scaled.reshape(k // 512, 128, 4, n).transpose(0, 1, 3, 2))
    if fmt == "e4m3":
        words = by_word.astype(ml_dtypes.float8_e4m3fn).view(np.uint8)
    else:
        c = by_word.astype(ml_dtypes.float4_e2m1fn).view(np.uint8) & 0xF
        words = c[..., 0::2] | (c[..., 1::2] << 4)
    return np.ascontiguousarray(words), np.ascontiguousarray(byte.astype(np.uint8).reshape(k // 512, 16, n))


def unpack_weight(words, scales, fmt):
    g, p, n, _ = words.shape
    if fmt == "e4m3":
        vals = np.ascontiguousarray(words).view(ml_dtypes.float8_e4m3fn).astype(np.float64)
    else:
        nib = np.empty((g, p, n, 4), np.uint8)
        nib[..., 0::2] = words & 0xF
        nib[..., 1::2] = words >> 4
        vals = E2M1[nib]
    vals = vals * np.repeat(np.exp2(scales.astype(np.float64) - 127.0), 8, axis=1)[..., None]
    return vals.transpose(0, 1, 3, 2).reshape(g * 512, n)

def pack4(w):
    words, scales = pack_weight(w, "e2m1")
    return words.reshape(words.shape[0], 128, -1), scales


def unpack4(words, scales):
    return unpack_weight(words.reshape(words.shape[0], 128, -1, 2), scales, "e2m1")


N, DIN, DOUT = 4096, 1024, 1024
C = 1.0
MIN_NORM = 1e-15
EPS_PROJ = 4e-3


def safe_norm(v):
    return np.sqrt(np.maximum(np.sum(v * v, axis=-1, keepdims=True), MIN_NORM))


def artanh(u):
    u = np.clip(u, -1.0 + 1e-5, 1.0 - 1e-5)
    return 0.5 * np.log((1.0 + u) / (1.0 - u))


def project(v, c):
    norm = safe_norm(v)
    maxnorm = (1.0 - EPS_PROJ) / np.sqrt(c)
    return np.where(norm > maxnorm, v / norm * maxnorm, v)


def mobius_matvec(W, x, c):
    sqc = np.sqrt(c)
    x_norm = safe_norm(x)
    mx = mxq(x, 1, "e4m3") @ W.T
    mx_norm = safe_norm(mx)
    res = np.tanh(mx_norm / x_norm * artanh(sqc * x_norm)) * mx / (mx_norm * sqc)
    zero = np.all(mx == 0, axis=-1, keepdims=True)
    return np.where(zero, 0.0, res)


def expmap0(u, c):
    sqc = np.sqrt(c)
    u_norm = safe_norm(u)
    return np.tanh(sqc * u_norm) * u / (sqc * u_norm)


def mobius_add(x, y, c):
    x2 = np.sum(x * x, axis=-1, keepdims=True)
    y2 = np.sum(y * y, axis=-1, keepdims=True)
    xy = np.sum(x * y, axis=-1, keepdims=True)
    num = (1.0 + 2.0 * c * xy + c * y2) * x + (1.0 - c * x2) * y
    denom = 1.0 + 2.0 * c * xy + c * c * x2 * y2
    return num / np.maximum(denom, MIN_NORM)


def setup_inputs():
    s = mx_kscale(DIN)
    gain = np.sqrt(np.mean(s * s))
    lim = 2.0 * np.sqrt(6.0 / (DIN + DOUT))
    m = np.random.standard_normal(DIN)
    g = (np.random.standard_normal((N, DIN)) + 0.5 * m) * s
    r = 0.3 + 0.68 * np.random.random_sample((N, 1))
    w0 = np.random.uniform(-lim, lim, (DOUT, DIN))
    wm = w0 @ m
    b = wm / np.linalg.norm(wm) + np.random.standard_normal(DOUT) / np.sqrt(DOUT)
    words, scales = pack4((w0 * gain / s).T)
    return {"x": bf(g / np.linalg.norm(g, axis=-1, keepdims=True) * r), "weight_words": words, "weight_scales": scales, "bias": bf(0.35 * b)}


def reference(x, weight_words, weight_scales, bias):
    c = C
    res = mobius_matvec(unpack4(weight_words, weight_scales).T, f64(x), c)
    res = project(res, c)
    hyp_bias = project(expmap0(f64(bias)[None, :], c), c)
    res = project(mobius_add(res, hyp_bias, c), c)
    return res

@@ -1,0 +1,289 @@
+from contextlib import ExitStack
+
+import concourse.bass as bass
+import concourse.mybir as mybir
+import concourse.tile as tile
+from concourse.masks import make_identity
+
+F32 = mybir.dt.float32
+BF16 = mybir.dt.bfloat16
+U8 = mybir.dt.uint8
+U32 = mybir.dt.uint32
+I32 = mybir.dt.int32
+FP8X4 = mybir.dt.float8_e4m3fn_x4
+FP4X4 = mybir.dt.float4_e2m1fn_x4
+AL = mybir.AluOpType
+AF = mybir.ActivationFunctionType
+
+P = 128
+ROWS = 4096
+K = 1024
+N = 1024
+NT = ROWS // P
+HALF = 512
+FLOPS = 2 * ROWS * K * N
+
+CHUNKS = [1, 1, 2, 4, 4, 4, 4, 4, 4, 4]
+GROUPS = [2, 2, 2, 2, 2, 2, 2, 1, 1]
+LAG = 4
+MAXN = 0.996
+C2 = MAXN * MAXN
+
+
+def tile_hyplinear_kernel(tc, x, weight_words, weight_scales, bias, out):
+    nc = tc.nc
+    x_v = x.rearrange("(p t) k -> p t k", t=NT)
+    out_v = out.rearrange("(p t) n -> p t n", t=NT)
+
+    with ExitStack() as ctx:
+        keep = ctx.enter_context(tc.tile_pool(name="keep", bufs=1))
+        grp_pool = ctx.enter_context(tc.tile_pool(name="grp", bufs=3))
+        junk = ctx.enter_context(tc.tile_pool(name="junk", bufs=2))
+        st = ctx.enter_context(tc.tile_pool(name="st", bufs=3))
+        bb_pool = ctx.enter_context(tc.tile_pool(name="bb", bufs=3))
+        o_pool = ctx.enter_context(tc.tile_pool(name="o", bufs=4))
+        ps_t = ctx.enter_context(tc.psum_pool(name="ps_t", bufs=2))
+        ps_m = ctx.enter_context(tc.psum_pool(name="ps_m", bufs=6))
+
+        wsc = keep.tile([P, 2, N], U8, align_bytes=64)
+        nc.vector.memset(wsc[:].bitcast(I32), 0)
+        halfc = keep.tile([P, 8], F32)
+        nc.vector.memset(halfc[:], 0.5)
+        mhalfc = keep.tile([P, 8], F32)
+        nc.vector.memset(mhalfc[:], -0.5)
+        ident = keep.tile([P, P], F32)
+        make_identity(nc, ident[:])
+
+        xc = []
+        t0 = 0
+        tile_loc = []
+        for ci, cn in enumerate(CHUNKS):
+            xt_sb = keep.tile([P, cn, K], BF16, name="xc%d" % ci)
+            xc.append(xt_sb)
+            for k in range(cn):
+                tile_loc.append((ci, k))
+            t0 += cn
+
+        def load_chunk(ci):
+            s = sum(CHUNKS[:ci])
+            nc.sync.dma_start(out=xc[ci][:], in_=x_v[:, s : s + CHUNKS[ci], :])
+
+        load_chunk(0)
+        ws32 = weight_scales.bitcast(I32)
+        for q in range(4):
+            nc.sync.dma_start(
+                out=wsc[32 * q : 32 * q + 4].bitcast(I32),
+                in_=ws32[:, 4 * q : 4 * q + 4, :].rearrange("g r n -> r g n"),
+            )
+        wq = keep.tile([P, 2, 2 * N], U8, align_bytes=64)
+        nc.sync.dma_start(out=wq[:].bitcast(I32), in_=weight_words.bitcast(I32).rearrange("g p n -> p g n"))
+        b_bc = keep.tile([P, N], BF16)
+        nc.scalar.dma_start(out=b_bc[:], in_=bias.partition_broadcast(P))
+        for ci in range(1, len(CHUNKS)):
+            load_chunk(ci)
+
+        xq = keep.tile([P, NT, 256], U32, align_bytes=64)
+        xs = keep.tile([P, NT, 256], U8, align_bytes=64)
+        sx_all = keep.tile([P, NT], F32)
+        sq_all = keep.tile([P, NT, 2], F32)
+        d_all = keep.tile([P, NT, 2], F32)
+        a_all = keep.tile([P, NT], F32)
+        b_all = keep.tile([P, NT], F32)
+
+        jb = junk.tile([P, N], BF16, name="jx")
+        sb = keep.tile([P, 1], F32)
+        nc.scalar.activation(out=jb[:], in_=b_bc[:], func=AF.Square, accum_out=sb[:])
+        sbc = keep.tile([P, 1], F32)
+        nc.vector.tensor_scalar_max(out=sbc[:], in0=sb[:], scalar1=1e-15)
+        bn = keep.tile([P, 1], F32)
+        nc.gpsimd.tensor_tensor(out=bn[:], in0=sbc[:], in1=halfc[:, 0:1], op=AL.pow)
+        tb = keep.tile([P, 1], F32)
+        nc.scalar.activation(out=tb[:], in_=bn[:], func=AF.Tanh)
+        rbn = keep.tile([P, 1], F32)
+        nc.vector.reciprocal(out=rbn[:], in_=bn[:])
+        hh = keep.tile([P, 1], F32)
+        nc.vector.scalar_tensor_tensor(out=hh[:], in0=tb[:], scalar=MAXN, in1=rbn[:], op0=AL.min, op1=AL.mult)
+        h2 = keep.tile([P, 1], F32)
+        nc.vector.tensor_scalar_mul(out=h2[:], in0=hh[:], scalar1=2.0)
+        nh = keep.tile([P, 1], F32)
+        nc.vector.tensor_scalar_mul(out=nh[:], in0=hh[:], scalar1=-1.0)
+        hsq = keep.tile([P, 1], F32)
+        nc.vector.tensor_tensor(out=hsq[:], in0=hh[:], in1=hh[:], op=AL.mult)
+        y2 = keep.tile([P, 1], F32)
+        nc.vector.tensor_tensor(out=y2[:], in0=hsq[:], in1=sb[:], op=AL.mult)
+        y2p1 = keep.tile([P, 1], F32)
+        nc.vector.tensor_scalar_add(out=y2p1[:], in0=y2[:], scalar1=1.0)
+        k1c = keep.tile([P, 1], F32)
+        nc.vector.tensor_scalar(out=k1c[:], in0=y2[:], scalar1=-1.0 / C2, scalar2=1.0 / C2, op0=AL.mult, op1=AL.add)
+
+        def stage_x(s):
+            grp = grp_pool.tile([P, 2, K], BF16, name="grp", align_bytes=64)
+            xts = []
+            for j in range(2):
+                ci, k = tile_loc[2 * s + j]
+                xw = xc[ci][:, k, :].bitcast(F32)
+                xt = ps_t.tile([P, 4, P], F32, name="xt")
+                xts.append(xt)
+                for g in range(2):
+                    for u in range(2):
+                        nc.tensor.transpose(xt[:, 2 * g + u, :], xw[:, 256 * g + u : 256 * (g + 1) : 2], ident[:])
+            for j in range(2):
+                dst = grp[:, j, :].bitcast(F32).rearrange("p (g r u) -> p g r u", g=2, u=2)
+                src = xts[j][:].rearrange("p (g u) r -> p g r u", g=2)
+                if j == 1 and s % 2 == 1:
+                    nc.vector.tensor_copy(out=dst, in_=src)
+                else:
+                    nc.scalar.copy(out=dst, in_=src)
+            return grp
+
+        def quant(s, grp):
+            nc.vector.quantize_mx(
+                out=xq[:, 2 * s : 2 * s + 2, :].rearrange("p a c -> p (a c)").bitcast(FP8X4),
+                scales=xs[:, 2 * s : 2 * s + 2, :].rearrange("p a c -> p (a c)"),
+                in_=grp[:].rearrange("p a c -> p (a c)"),
+            )
+
+        def xnorm(t):
+            ci, k = tile_loc[t]
+            jx = junk.tile([P, K], BF16, name="jx")
+            nc.scalar.activation(out=jx[:], in_=xc[ci][:, k, :], func=AF.Square, accum_out=sx_all[:, t : t + 1])
+
+        def mm(t):
+            accs = []
+            for h in range(2):
+                acc = ps_m.tile([P, HALF], F32, name="acc")
+                accs.append(acc)
+            for g in range(2):
+                for h in range(2):
+                    nc.tensor.matmul_mx(
+                        out=accs[h][:],
+                        lhsT=xq[:, t, P * g : P * (g + 1)].bitcast(FP8X4),
+                        lhsT_scale=xs[:, t, P * g : P * (g + 1)],
+                        rhs=wq[:, g, 2 * HALF * h : 2 * HALF * (h + 1)].bitcast(FP4X4),
+                        rhs_scale=wsc[:, g, HALF * h : HALF * (h + 1)],
+                        start=(g == 0),
+                        stop=(g == 1),
+                    )
+            return accs
+
+        def sq(t, h, acc):
+            js = junk.tile([P, HALF], BF16, name="js")
+            nc.scalar.activation(out=js[:], in_=acc[:], func=AF.Square, accum_out=sq_all[:, t, h : h + 1])
+
+        def dot(t, h, acc):
+            jv = junk.tile([P, HALF], F32, name="jv")
+            nc.vector.scalar_tensor_tensor(
+                out=jv[:], in0=acc[:], scalar=1.0, in1=b_bc[:, HALF * h : HALF * (h + 1)],
+                op0=AL.mult, op1=AL.mult, accum_out=d_all[:, t, h : h + 1],
+            )
+
+        def stage_m1(t):
+            accs = mm(t)
+            sq(t, 0, accs[0])
+            dot(t, 1, accs[1])
+            sq(t, 1, accs[1])
+            dot(t, 0, accs[0])
+
+        def chain(s, n):
+            sl = slice(s, s + n)
+            V = nc.vector
+
+            def T(nm):
+                return st.tile([P, n], F32, name=nm)
+
+            sxc = T("sxc")
+            V.tensor_scalar_max(out=sxc[:], in0=sx_all[:, sl], scalar1=1e-15)
+            xn = T("xn")
+            nc.gpsimd.tensor_tensor(out=xn[:], in0=sxc[:], in1=halfc[:, :n], op=AL.pow)
+            smc = T("smc")
+            V.scalar_tensor_tensor(out=smc[:], in0=sq_all[:, sl, 0], scalar=1e-15, in1=sq_all[:, sl, 1], op0=AL.max, op1=AL.add)
+            mn = T("mn")
+            nc.gpsimd.tensor_tensor(out=mn[:], in0=smc[:], in1=halfc[:, :n], op=AL.pow)
+            dd = T("dd")
+            V.tensor_tensor(out=dd[:], in0=d_all[:, sl, 0], in1=d_all[:, sl, 1], op=AL.add)
+            uu = T("uu")
+            V.tensor_scalar_min(out=uu[:], in0=xn[:], scalar1=1.0 - 1e-5)
+            om = T("om")
+            V.tensor_scalar(out=om[:], in0=uu[:], scalar1=-1.0, scalar2=1.0, op0=AL.mult, op1=AL.add)
+            rom = T("rom")
+            V.reciprocal(out=rom[:], in_=om[:])
+            ww = T("ww")
+            V.scalar_tensor_tensor(out=ww[:], in0=uu[:], scalar=1.0, in1=rom[:], op0=AL.add, op1=AL.mult)
+            rxn = T("rxn")
+            V.reciprocal(out=rxn[:], in_=xn[:])
+            qq = T("qq")
+            V.tensor_tensor(out=qq[:], in0=mn[:], in1=rxn[:], op=AL.mult)
+            ee = T("ee")
+            nc.gpsimd.tensor_tensor(out=ee[:], in0=ww[:], in1=qq[:], op=AL.pow)
+            rmn = T("rmn")
+            V.reciprocal(out=rmn[:], in_=mn[:])
+            e1 = T("e1")
+            V.tensor_scalar(out=e1[:], in0=ee[:], scalar1=1e30, scalar2=1.0, op0=AL.min, op1=AL.add)
+            re = T("re")
+            V.reciprocal(out=re[:], in_=e1[:])
+            m2 = T("m2")
+            V.tensor_scalar(out=m2[:], in0=re[:], scalar1=(1.0 - MAXN) / 2.0, scalar2=-2.0, op0=AL.max, op1=AL.mult)
+            rho = T("rho")
+            V.tensor_scalar_add(out=rho[:], in0=m2[:], scalar1=1.0)
+            nb = T("nb")
+            V.scalar_tensor_tensor(out=nb[:], in0=m2[:], scalar=2.0, in1=m2[:], op0=AL.add, op1=AL.mult)
+            c1 = T("c1")
+            V.tensor_tensor(out=c1[:], in0=rho[:], in1=rmn[:], op=AL.mult)
+            dx = T("dx")
+            V.scalar_tensor_tensor(out=dx[:], in0=dd[:], scalar=h2[:], in1=c1[:], op0=AL.mult, op1=AL.mult)
+            al = T("al")
+            V.tensor_scalar_add(out=al[:], in0=dx[:], scalar1=y2p1[:])
+            den = T("den")
+            V.scalar_tensor_tensor(out=den[:], in0=nb[:], scalar=y2[:], in1=al[:], op0=AL.mult, op1=AL.add)
+            rden = T("rden")
+            V.reciprocal(out=rden[:], in_=den[:])
+            gg = T("gg")
+            V.scalar_tensor_tensor(out=gg[:], in0=nb[:], scalar=k1c[:], in1=rden[:], op0=AL.mult, op1=AL.mult)
+            wv = T("wv")
+            V.tensor_scalar(out=wv[:], in0=gg[:], scalar1=1.0 / C2, scalar2=1.0, op0=AL.add, op1=AL.max)
+            ss = T("ss")
+            nc.gpsimd.tensor_tensor(out=ss[:], in0=wv[:], in1=mhalfc[:, :n], op=AL.pow)
+            ac = T("ac")
+            V.tensor_tensor(out=ac[:], in0=al[:], in1=c1[:], op=AL.mult)
+            ff = T("ff")
+            V.tensor_tensor(out=ff[:], in0=ss[:], in1=rden[:], op=AL.mult)
+            V.tensor_tensor(out=a_all[:, sl], in0=ac[:], in1=ff[:], op=AL.mult)
+            V.scalar_tensor_tensor(out=b_all[:, sl], in0=nb[:], scalar=nh[:], in1=ff[:], op0=AL.mult, op1=AL.mult)
+
+        def make_bb(t):
+            bb = bb_pool.tile([P, N], F32, name="bb")
+            nc.gpsimd.tensor_scalar(out=bb[:], in0=b_bc[:], scalar1=b_all[:, t : t + 1], scalar2=0.0, op0=AL.mult, op1=AL.add)
+            return bb
+
+        def stage_m2(t):
+            bb = make_bb(t)
+            accs = mm(t)
+            o = o_pool.tile([P, N], F32, name="o")
+            for h in range(2):
+                hs = slice(HALF * h, HALF * (h + 1))
+                nc.vector.scalar_tensor_tensor(
+                    out=o[:, hs], in0=accs[h][:], scalar=a_all[:, t : t + 1], in1=bb[:, hs], op0=AL.mult, op1=AL.add
+                )
+            nc.sync.dma_start(out=out_v[:, t, :], in_=o[:])
+
+        NP = NT // 2
+        group_end = {}
+        s0 = 0
+        for gp in GROUPS:
+            group_end[s0 + gp - 1] = (2 * s0, 2 * gp)
+            s0 += gp
+        for s in range(NP + LAG):
+            grp = None
+            if s < NP:
+                grp = stage_x(s)
+            for j in range(2):
+                if s < NP:
+                    xnorm(2 * s + j)
+                if 1 <= s <= NP:
+                    stage_m1(2 * (s - 1) + j)
+                if s >= LAG:
+                    stage_m2(2 * (s - LAG) + j)
+                if j == 0 and s < NP:
+                    quant(s, grp)
+            if (s - 1) in group_end:
+                chain(group_end[s - 1][0], group_end[s - 1][1])

@@ -24,7 +24,12 @@ HALF = 512
 FLOPS = 2 * ROWS * K * N
 
 CHUNKS = [1, 1, 2, 4, 4, 4, 4, 4, 4, 4]
-GROUPS = [2, 2, 2, 2, 2, 2, 2, 1, 1]
+GROUPS = [4, 4, 4, 4, 4, 4, 4, 2, 2]
+XGROUPS = [4, 4, 4, 4, 4, 4, 4, 2, 2]
+LX = 3
+M2_PER_STEP = 2
+M1_BANKS = 4
+M2_BANKS = 2
 LAG = 4
 MAXN = 0.996
 C2 = MAXN * MAXN
@@ -43,7 +48,8 @@ def tile_hyplinear_kernel(tc, x, weight_words, weight_scales, bias, out):
         bb_pool = ctx.enter_context(tc.tile_pool(name="bb", bufs=3))
         o_pool = ctx.enter_context(tc.tile_pool(name="o", bufs=4))
         ps_t = ctx.enter_context(tc.psum_pool(name="ps_t", bufs=2))
-        ps_m = ctx.enter_context(tc.psum_pool(name="ps_m", bufs=6))
+        ps_m = ctx.enter_context(tc.psum_pool(name="ps_m", bufs=M1_BANKS))
+        ps_o = ctx.enter_context(tc.psum_pool(name="ps_o", bufs=M2_BANKS))
 
         wsc = keep.tile([P, 2, N], U8, align_bytes=64)
         nc.vector.memset(wsc[:].bitcast(I32), 0)
@@ -89,6 +95,8 @@ def tile_hyplinear_kernel(tc, x, weight_words, weight_scales, bias, out):
         d_all = keep.tile([P, NT, 2], F32)
         a_all = keep.tile([P, NT], F32)
         b_all = keep.tile([P, NT], F32)
+        rxn_all = keep.tile([P, NT], F32)
+        w_all = keep.tile([P, NT], F32)
 
         jb = junk.tile([P, N], BF16, name="jx")
         sb = keep.tile([P, 1], F32)
@@ -111,6 +119,8 @@ def tile_hyplinear_kernel(tc, x, weight_words, weight_scales, bias, out):
         nc.vector.tensor_tensor(out=hsq[:], in0=hh[:], in1=hh[:], op=AL.mult)
         y2 = keep.tile([P, 1], F32)
         nc.vector.tensor_tensor(out=y2[:], in0=hsq[:], in1=sb[:], op=AL.mult)
+        ny2 = keep.tile([P, 1], F32)
+        nc.vector.tensor_scalar_mul(out=ny2[:], in0=y2[:], scalar1=-1.0)
         y2p1 = keep.tile([P, 1], F32)
         nc.vector.tensor_scalar_add(out=y2p1[:], in0=y2[:], scalar1=1.0)
         k1c = keep.tile([P, 1], F32)
@@ -130,7 +140,7 @@ def tile_hyplinear_kernel(tc, x, weight_words, weight_scales, bias, out):
             for j in range(2):
                 dst = grp[:, j, :].bitcast(F32).rearrange("p (g r u) -> p g r u", g=2, u=2)
                 src = xts[j][:].rearrange("p (g u) r -> p g r u", g=2)
-                if j == 1 and s % 2 == 1:
+                if s < 3:
                     nc.vector.tensor_copy(out=dst, in_=src)
                 else:
                     nc.scalar.copy(out=dst, in_=src)
@@ -148,10 +158,10 @@ def tile_hyplinear_kernel(tc, x, weight_words, weight_scales, bias, out):
             jx = junk.tile([P, K], BF16, name="jx")
             nc.scalar.activation(out=jx[:], in_=xc[ci][:, k, :], func=AF.Square, accum_out=sx_all[:, t : t + 1])
 
-        def mm(t):
+        def mm(t, pool):
             accs = []
             for h in range(2):
-                acc = ps_m.tile([P, HALF], F32, name="acc")
+                acc = pool.tile([P, HALF], F32, name="acc")
                 accs.append(acc)
             for g in range(2):
                 for h in range(2):
@@ -178,11 +188,27 @@ def tile_hyplinear_kernel(tc, x, weight_words, weight_scales, bias, out):
             )
 
         def stage_m1(t):
-            accs = mm(t)
+            accs = mm(t, ps_m)
             sq(t, 0, accs[0])
             dot(t, 1, accs[1])
             sq(t, 1, accs[1])
             dot(t, 0, accs[0])
+
+        def chain_x(s, n):
+            sl = slice(s, s + n)
+            V = nc.vector
+            sxc = st.tile([P, n], F32, name="sxc%d" % n)
+            V.tensor_scalar_max(out=sxc[:], in0=sx_all[:, sl], scalar1=1e-15)
+            xn = st.tile([P, n], F32, name="xn%d" % n)
+            nc.scalar.activation(out=xn[:], in_=sxc[:], func=AF.Sqrt)
+            uu = st.tile([P, n], F32, name="uu%d" % n)
+            V.tensor_scalar_min(out=uu[:], in0=xn[:], scalar1=1.0 - 1e-5)
+            V.reciprocal(out=rxn_all[:, sl], in_=xn[:])
+            om = st.tile([P, n], F32, name="om%d" % n)
+            V.tensor_scalar(out=om[:], in0=uu[:], scalar1=-1.0, scalar2=1.0, op0=AL.mult, op1=AL.add)
+            rom = st.tile([P, n], F32, name="rom%d" % n)
+            V.reciprocal(out=rom[:], in_=om[:])
+            V.scalar_tensor_tensor(out=w_all[:, sl], in0=uu[:], scalar=1.0, in1=rom[:], op0=AL.add, op1=AL.mult)
 
         def chain(s, n):
             sl = slice(s, s + n)
@@ -191,30 +217,16 @@ def tile_hyplinear_kernel(tc, x, weight_words, weight_scales, bias, out):
             def T(nm):
                 return st.tile([P, n], F32, name=nm)
 
-            sxc = T("sxc")
-            V.tensor_scalar_max(out=sxc[:], in0=sx_all[:, sl], scalar1=1e-15)
-            xn = T("xn")
-            nc.gpsimd.tensor_tensor(out=xn[:], in0=sxc[:], in1=halfc[:, :n], op=AL.pow)
             smc = T("smc")
             V.scalar_tensor_tensor(out=smc[:], in0=sq_all[:, sl, 0], scalar=1e-15, in1=sq_all[:, sl, 1], op0=AL.max, op1=AL.add)
             mn = T("mn")
-            nc.gpsimd.tensor_tensor(out=mn[:], in0=smc[:], in1=halfc[:, :n], op=AL.pow)
+            nc.scalar.activation(out=mn[:], in_=smc[:], func=AF.Sqrt)
             dd = T("dd")
             V.tensor_tensor(out=dd[:], in0=d_all[:, sl, 0], in1=d_all[:, sl, 1], op=AL.add)
-            uu = T("uu")
-            V.tensor_scalar_min(out=uu[:], in0=xn[:], scalar1=1.0 - 1e-5)
-            om = T("om")
-            V.tensor_scalar(out=om[:], in0=uu[:], scalar1=-1.0, scalar2=1.0, op0=AL.mult, op1=AL.add)
-            rom = T("rom")
-            V.reciprocal(out=rom[:], in_=om[:])
-            ww = T("ww")
-            V.scalar_tensor_tensor(out=ww[:], in0=uu[:], scalar=1.0, in1=rom[:], op0=AL.add, op1=AL.mult)
-            rxn = T("rxn")
-            V.reciprocal(out=rxn[:], in_=xn[:])
             qq = T("qq")
-            V.tensor_tensor(out=qq[:], in0=mn[:], in1=rxn[:], op=AL.mult)
+            V.tensor_tensor(out=qq[:], in0=mn[:], in1=rxn_all[:, sl], op=AL.mult)
             ee = T("ee")
-            nc.gpsimd.tensor_tensor(out=ee[:], in0=ww[:], in1=qq[:], op=AL.pow)
+            nc.gpsimd.tensor_tensor(out=ee[:], in0=w_all[:, sl], in1=qq[:], op=AL.pow)
             rmn = T("rmn")
             V.reciprocal(out=rmn[:], in_=mn[:])
             e1 = T("e1")
@@ -223,32 +235,34 @@ def tile_hyplinear_kernel(tc, x, weight_words, weight_scales, bias, out):
             V.reciprocal(out=re[:], in_=e1[:])
             m2 = T("m2")
             V.tensor_scalar(out=m2[:], in0=re[:], scalar1=(1.0 - MAXN) / 2.0, scalar2=-2.0, op0=AL.max, op1=AL.mult)
-            rho = T("rho")
-            V.tensor_scalar_add(out=rho[:], in0=m2[:], scalar1=1.0)
             nb = T("nb")
             V.scalar_tensor_tensor(out=nb[:], in0=m2[:], scalar=2.0, in1=m2[:], op0=AL.add, op1=AL.mult)
             c1 = T("c1")
-            V.tensor_tensor(out=c1[:], in0=rho[:], in1=rmn[:], op=AL.mult)
+            V.scalar_tensor_tensor(out=c1[:], in0=m2[:], scalar=1.0, in1=rmn[:], op0=AL.add, op1=AL.mult)
+            u1 = T("u1")
+            V.tensor_scalar(out=u1[:], in0=nb[:], scalar1=y2[:], scalar2=y2p1[:], op0=AL.mult, op1=AL.add)
             dx = T("dx")
             V.scalar_tensor_tensor(out=dx[:], in0=dd[:], scalar=h2[:], in1=c1[:], op0=AL.mult, op1=AL.mult)
-            al = T("al")
-            V.tensor_scalar_add(out=al[:], in0=dx[:], scalar1=y2p1[:])
             den = T("den")
-            V.scalar_tensor_tensor(out=den[:], in0=nb[:], scalar=y2[:], in1=al[:], op0=AL.mult, op1=AL.add)
+            V.tensor_tensor(out=den[:], in0=u1[:], in1=dx[:], op=AL.add)
             rden = T("rden")
             V.reciprocal(out=rden[:], in_=den[:])
-            gg = T("gg")
-            V.scalar_tensor_tensor(out=gg[:], in0=nb[:], scalar=k1c[:], in1=rden[:], op0=AL.mult, op1=AL.mult)
+            nt = T("nt")
+            V.tensor_tensor(out=nt[:], in0=nb[:], in1=rden[:], op=AL.mult)
             wv = T("wv")
-            V.tensor_scalar(out=wv[:], in0=gg[:], scalar1=1.0 / C2, scalar2=1.0, op0=AL.add, op1=AL.max)
-            ss = T("ss")
-            nc.gpsimd.tensor_tensor(out=ss[:], in0=wv[:], in1=mhalfc[:, :n], op=AL.pow)
-            ac = T("ac")
-            V.tensor_tensor(out=ac[:], in0=al[:], in1=c1[:], op=AL.mult)
-            ff = T("ff")
-            V.tensor_tensor(out=ff[:], in0=ss[:], in1=rden[:], op=AL.mult)
-            V.tensor_tensor(out=a_all[:, sl], in0=ac[:], in1=ff[:], op=AL.mult)
-            V.scalar_tensor_tensor(out=b_all[:, sl], in0=nb[:], scalar=nh[:], in1=ff[:], op0=AL.mult, op1=AL.mult)
+            V.tensor_scalar(out=wv[:], in0=nt[:], scalar1=k1c[:], scalar2=1.0 / C2 - 1.0, op0=AL.mult, op1=AL.add)
+            wr = T("wr")
+            nc.scalar.activation(out=wr[:], in_=wv[:], func=AF.Relu)
+            sw = T("sw")
+            nc.scalar.activation(out=sw[:], in_=wr[:], func=AF.Sqrt, bias=1.0)
+            a1 = T("a1")
+            V.tensor_scalar(out=a1[:], in0=nt[:], scalar1=ny2[:], scalar2=1.0, op0=AL.mult, op1=AL.add)
+            a2 = T("a2")
+            V.tensor_tensor(out=a2[:], in0=a1[:], in1=c1[:], op=AL.mult)
+            rs = T("rs")
+            V.reciprocal(out=rs[:], in_=sw[:])
+            V.tensor_tensor(out=a_all[:, sl], in0=a2[:], in1=rs[:], op=AL.mult)
+            V.scalar_tensor_tensor(out=b_all[:, sl], in0=nt[:], scalar=nh[:], in1=rs[:], op0=AL.mult, op1=AL.mult)
 
         def make_bb(t):
             bb = bb_pool.tile([P, N], F32, name="bb")
@@ -257,7 +271,7 @@ def tile_hyplinear_kernel(tc, x, weight_words, weight_scales, bias, out):
 
         def stage_m2(t):
             bb = make_bb(t)
-            accs = mm(t)
+            accs = mm(t, ps_o)
             o = o_pool.tile([P, N], F32, name="o")
             for h in range(2):
                 hs = slice(HALF * h, HALF * (h + 1))
@@ -266,24 +280,37 @@ def tile_hyplinear_kernel(tc, x, weight_words, weight_scales, bias, out):
                 )
             nc.sync.dma_start(out=out_v[:, t, :], in_=o[:])
 
-        NP = NT // 2
-        group_end = {}
-        s0 = 0
-        for gp in GROUPS:
-            group_end[s0 + gp - 1] = (2 * s0, 2 * gp)
-            s0 += gp
-        for s in range(NP + LAG):
-            grp = None
-            if s < NP:
-                grp = stage_x(s)
-            for j in range(2):
-                if s < NP:
-                    xnorm(2 * s + j)
-                if 1 <= s <= NP:
-                    stage_m1(2 * (s - 1) + j)
-                if s >= LAG:
-                    stage_m2(2 * (s - LAG) + j)
-                if j == 0 and s < NP:
-                    quant(s, grp)
-            if (s - 1) in group_end:
-                chain(group_end[s - 1][0], group_end[s - 1][1])
+        last_of_group = {}
+        g0 = 0
+        for gn in GROUPS:
+            last_of_group[g0 + gn - 1] = (g0, gn)
+            g0 += gn
+        last_of_xgroup = {}
+        g0 = 0
+        for gn in XGROUPS:
+            last_of_xgroup[g0 + gn - 1] = (g0, gn)
+            g0 += gn
+        ready = 0
+        done2 = 0
+        i = 0
+        grp = None
+        while done2 < NT:
+            a = i - LX
+            if i % 2 == 0 and i < NT:
+                grp = stage_x(i // 2)
+            if i < NT:
+                xnorm(i)
+            if i in last_of_xgroup:
+                chain_x(last_of_xgroup[i][0], last_of_xgroup[i][1])
+            if 0 <= a < NT:
+                stage_m1(a)
+            for q in range(M2_PER_STEP):
+                if done2 < ready:
+                    stage_m2(done2)
+                    done2 += 1
+            if i % 2 == 0 and i < NT:
+                quant(i // 2, grp)
+            if a in last_of_group:
+                chain(last_of_group[a][0], last_of_group[a][1])
+                ready = a + 1
+            i += 1

@@ -24,8 +24,8 @@ HALF = 512
 FLOPS = 2 * ROWS * K * N
 
 CHUNKS = [1, 1, 2, 4, 4, 4, 4, 4, 4, 4]
-GROUPS = [4, 4, 4, 4, 4, 4, 4, 2, 2]
-XGROUPS = [4, 4, 4, 4, 4, 4, 4, 2, 2]
+GROUPS = [4, 8, 8, 6, 4, 2]
+XGROUPS = [4, 8, 8, 6, 4, 2]
 LX = 3
 M2_PER_STEP = 2
 M1_BANKS = 4
@@ -45,7 +45,7 @@ def tile_hyplinear_kernel(tc, x, weight_words, weight_scales, bias, out):
         grp_pool = ctx.enter_context(tc.tile_pool(name="grp", bufs=3))
         junk = ctx.enter_context(tc.tile_pool(name="junk", bufs=2))
         st = ctx.enter_context(tc.tile_pool(name="st", bufs=3))
-        bb_pool = ctx.enter_context(tc.tile_pool(name="bb", bufs=3))
+        bb_pool = ctx.enter_context(tc.tile_pool(name="bb", bufs=4))
         o_pool = ctx.enter_context(tc.tile_pool(name="o", bufs=4))
         ps_t = ctx.enter_context(tc.psum_pool(name="ps_t", bufs=2))
         ps_m = ctx.enter_context(tc.psum_pool(name="ps_m", bufs=M1_BANKS))
@@ -140,7 +140,7 @@ def tile_hyplinear_kernel(tc, x, weight_words, weight_scales, bias, out):
             for j in range(2):
                 dst = grp[:, j, :].bitcast(F32).rearrange("p (g r u) -> p g r u", g=2, u=2)
                 src = xts[j][:].rearrange("p (g u) r -> p g r u", g=2)
-                if s < 3:
+                if s < 6:
                     nc.vector.tensor_copy(out=dst, in_=src)
                 else:
                     nc.scalar.copy(out=dst, in_=src)
@@ -196,77 +196,91 @@ def tile_hyplinear_kernel(tc, x, weight_words, weight_scales, bias, out):
 
         def chain_x(s, n):
             sl = slice(s, s + n)
-            V = nc.vector
+            G = nc.gpsimd
             sxc = st.tile([P, n], F32, name="sxc%d" % n)
-            V.tensor_scalar_max(out=sxc[:], in0=sx_all[:, sl], scalar1=1e-15)
+            G.tensor_scalar_max(out=sxc[:], in0=sx_all[:, sl], scalar1=1e-15)
             xn = st.tile([P, n], F32, name="xn%d" % n)
             nc.scalar.activation(out=xn[:], in_=sxc[:], func=AF.Sqrt)
-            uu = st.tile([P, n], F32, name="uu%d" % n)
-            V.tensor_scalar_min(out=uu[:], in0=xn[:], scalar1=1.0 - 1e-5)
-            V.reciprocal(out=rxn_all[:, sl], in_=xn[:])
+            nc.vector.reciprocal(out=rxn_all[:, sl], in_=xn[:])
             om = st.tile([P, n], F32, name="om%d" % n)
-            V.tensor_scalar(out=om[:], in0=uu[:], scalar1=-1.0, scalar2=1.0, op0=AL.mult, op1=AL.add)
+            G.tensor_scalar(out=om[:], in0=xn[:], scalar1=1.0 - 1e-5, scalar2=-1.0, op0=AL.min, op1=AL.add)
             rom = st.tile([P, n], F32, name="rom%d" % n)
-            V.reciprocal(out=rom[:], in_=om[:])
-            V.scalar_tensor_tensor(out=w_all[:, sl], in0=uu[:], scalar=1.0, in1=rom[:], op0=AL.add, op1=AL.mult)
+            nc.vector.reciprocal(out=rom[:], in_=om[:])
+            up = st.tile([P, n], F32, name="up%d" % n)
+            G.tensor_scalar(out=up[:], in0=om[:], scalar1=-1.0, scalar2=-2.0, op0=AL.mult, op1=AL.add)
+            G.tensor_tensor(out=w_all[:, sl], in0=up[:], in1=rom[:], op=AL.mult)
 
         def chain(s, n):
             sl = slice(s, s + n)
             V = nc.vector
+            G = nc.gpsimd
 
             def T(nm):
                 return st.tile([P, n], F32, name=nm)
 
+            sm = T("sm")
+            G.tensor_tensor(out=sm[:], in0=sq_all[:, sl, 0], in1=sq_all[:, sl, 1], op=AL.add)
             smc = T("smc")
-            V.scalar_tensor_tensor(out=smc[:], in0=sq_all[:, sl, 0], scalar=1e-15, in1=sq_all[:, sl, 1], op0=AL.max, op1=AL.add)
+            G.tensor_scalar_max(out=smc[:], in0=sm[:], scalar1=1e-15)
             mn = T("mn")
             nc.scalar.activation(out=mn[:], in_=smc[:], func=AF.Sqrt)
-            dd = T("dd")
-            V.tensor_tensor(out=dd[:], in0=d_all[:, sl, 0], in1=d_all[:, sl, 1], op=AL.add)
             qq = T("qq")
-            V.tensor_tensor(out=qq[:], in0=mn[:], in1=rxn_all[:, sl], op=AL.mult)
+            G.tensor_tensor(out=qq[:], in0=mn[:], in1=rxn_all[:, sl], op=AL.mult)
             ee = T("ee")
-            nc.gpsimd.tensor_tensor(out=ee[:], in0=w_all[:, sl], in1=qq[:], op=AL.pow)
+            G.tensor_tensor(out=ee[:], in0=w_all[:, sl], in1=qq[:], op=AL.pow)
             rmn = T("rmn")
             V.reciprocal(out=rmn[:], in_=mn[:])
             e1 = T("e1")
-            V.tensor_scalar(out=e1[:], in0=ee[:], scalar1=1e30, scalar2=1.0, op0=AL.min, op1=AL.add)
+            G.tensor_scalar(out=e1[:], in0=ee[:], scalar1=1e30, scalar2=1.0, op0=AL.min, op1=AL.add)
             re = T("re")
             V.reciprocal(out=re[:], in_=e1[:])
+            dd = T("dd")
+            G.tensor_tensor(out=dd[:], in0=d_all[:, sl, 0], in1=d_all[:, sl, 1], op=AL.add)
+            dh = T("dh")
+            G.tensor_scalar(out=dh[:], in0=dd[:], scalar1=h2[:], scalar2=0.0, op0=AL.mult, op1=AL.add)
             m2 = T("m2")
-            V.tensor_scalar(out=m2[:], in0=re[:], scalar1=(1.0 - MAXN) / 2.0, scalar2=-2.0, op0=AL.max, op1=AL.mult)
-            nb = T("nb")
-            V.scalar_tensor_tensor(out=nb[:], in0=m2[:], scalar=2.0, in1=m2[:], op0=AL.add, op1=AL.mult)
+            G.tensor_scalar(out=m2[:], in0=re[:], scalar1=(1.0 - MAXN) / 2.0, scalar2=-2.0, op0=AL.max, op1=AL.mult)
+            p1 = T("p1")
+            G.tensor_scalar_add(out=p1[:], in0=m2[:], scalar1=1.0)
             c1 = T("c1")
-            V.scalar_tensor_tensor(out=c1[:], in0=m2[:], scalar=1.0, in1=rmn[:], op0=AL.add, op1=AL.mult)
-            u1 = T("u1")
-            V.tensor_scalar(out=u1[:], in0=nb[:], scalar1=y2[:], scalar2=y2p1[:], op0=AL.mult, op1=AL.add)
+            G.tensor_tensor(out=c1[:], in0=p1[:], in1=rmn[:], op=AL.mult)
             dx = T("dx")
-            V.scalar_tensor_tensor(out=dx[:], in0=dd[:], scalar=h2[:], in1=c1[:], op0=AL.mult, op1=AL.mult)
+            G.tensor_tensor(out=dx[:], in0=dh[:], in1=c1[:], op=AL.mult)
+            p2 = T("p2")
+            G.tensor_scalar_add(out=p2[:], in0=m2[:], scalar1=2.0)
+            nb = T("nb")
+            G.tensor_tensor(out=nb[:], in0=p2[:], in1=m2[:], op=AL.mult)
+            u1 = T("u1")
+            G.tensor_scalar(out=u1[:], in0=nb[:], scalar1=y2[:], scalar2=y2p1[:], op0=AL.mult, op1=AL.add)
             den = T("den")
-            V.tensor_tensor(out=den[:], in0=u1[:], in1=dx[:], op=AL.add)
+            G.tensor_tensor(out=den[:], in0=u1[:], in1=dx[:], op=AL.add)
             rden = T("rden")
             V.reciprocal(out=rden[:], in_=den[:])
             nt = T("nt")
-            V.tensor_tensor(out=nt[:], in0=nb[:], in1=rden[:], op=AL.mult)
+            G.tensor_tensor(out=nt[:], in0=nb[:], in1=rden[:], op=AL.mult)
             wv = T("wv")
-            V.tensor_scalar(out=wv[:], in0=nt[:], scalar1=k1c[:], scalar2=1.0 / C2 - 1.0, op0=AL.mult, op1=AL.add)
+            G.tensor_scalar(out=wv[:], in0=nt[:], scalar1=k1c[:], scalar2=1.0 / C2 - 1.0, op0=AL.mult, op1=AL.add)
             wr = T("wr")
             nc.scalar.activation(out=wr[:], in_=wv[:], func=AF.Relu)
             sw = T("sw")
             nc.scalar.activation(out=sw[:], in_=wr[:], func=AF.Sqrt, bias=1.0)
-            a1 = T("a1")
-            V.tensor_scalar(out=a1[:], in0=nt[:], scalar1=ny2[:], scalar2=1.0, op0=AL.mult, op1=AL.add)
-            a2 = T("a2")
-            V.tensor_tensor(out=a2[:], in0=a1[:], in1=c1[:], op=AL.mult)
             rs = T("rs")
             V.reciprocal(out=rs[:], in_=sw[:])
-            V.tensor_tensor(out=a_all[:, sl], in0=a2[:], in1=rs[:], op=AL.mult)
-            V.scalar_tensor_tensor(out=b_all[:, sl], in0=nt[:], scalar=nh[:], in1=rs[:], op0=AL.mult, op1=AL.mult)
+            a1 = T("a1")
+            G.tensor_scalar(out=a1[:], in0=nt[:], scalar1=ny2[:], scalar2=1.0, op0=AL.mult, op1=AL.add)
+            a2 = T("a2")
+            G.tensor_tensor(out=a2[:], in0=a1[:], in1=c1[:], op=AL.mult)
+            bh = T("bh")
+            G.tensor_scalar(out=bh[:], in0=nt[:], scalar1=nh[:], scalar2=0.0, op0=AL.mult, op1=AL.add)
+            G.tensor_tensor(out=b_all[:, sl], in0=bh[:], in1=rs[:], op=AL.mult)
+            G.tensor_tensor(out=a_all[:, sl], in0=a2[:], in1=rs[:], op=AL.mult)
 
         def make_bb(t):
             bb = bb_pool.tile([P, N], F32, name="bb")
-            nc.gpsimd.tensor_scalar(out=bb[:], in0=b_bc[:], scalar1=b_all[:, t : t + 1], scalar2=0.0, op0=AL.mult, op1=AL.add)
+            if t >= 20:
+                nc.scalar.activation(out=bb[:], in_=b_bc[:], func=AF.Copy, scale=b_all[:, t : t + 1])
+            else:
+                nc.gpsimd.tensor_scalar(out=bb[:], in0=b_bc[:], scalar1=b_all[:, t : t + 1], scalar2=0.0, op0=AL.mult, op1=AL.add)
             return bb
 
         def stage_m2(t):

@@ -24,12 +24,12 @@ HALF = 512
 FLOPS = 2 * ROWS * K * N
 
 CHUNKS = [1, 1, 2, 4, 4, 4, 4, 4, 4, 4]
-GROUPS = [4, 8, 8, 6, 4, 2]
-XGROUPS = [4, 8, 8, 6, 4, 2]
+GROUPS = [4] * 8
+XGROUPS = [4] * 8
 LX = 3
-M2_PER_STEP = 2
+M2_PER_STEP = 1
 M1_BANKS = 4
-M2_BANKS = 2
+M2_BANKS = 3
 LAG = 4
 MAXN = 0.996
 C2 = MAXN * MAXN
@@ -45,9 +45,9 @@ def tile_hyplinear_kernel(tc, x, weight_words, weight_scales, bias, out):
         grp_pool = ctx.enter_context(tc.tile_pool(name="grp", bufs=3))
         junk = ctx.enter_context(tc.tile_pool(name="junk", bufs=2))
         st = ctx.enter_context(tc.tile_pool(name="st", bufs=3))
-        bb_pool = ctx.enter_context(tc.tile_pool(name="bb", bufs=4))
+        bb_pool = ctx.enter_context(tc.tile_pool(name="bb", bufs=3))
         o_pool = ctx.enter_context(tc.tile_pool(name="o", bufs=4))
-        ps_t = ctx.enter_context(tc.psum_pool(name="ps_t", bufs=2))
+        ps_t = ctx.enter_context(tc.psum_pool(name="ps_t", bufs=1))
         ps_m = ctx.enter_context(tc.psum_pool(name="ps_m", bufs=M1_BANKS))
         ps_o = ctx.enter_context(tc.psum_pool(name="ps_o", bufs=M2_BANKS))
 
@@ -163,8 +163,8 @@ def tile_hyplinear_kernel(tc, x, weight_words, weight_scales, bias, out):
             for h in range(2):
                 acc = pool.tile([P, HALF], F32, name="acc")
                 accs.append(acc)
-            for g in range(2):
-                for h in range(2):
+            for h in range(2):
+                for g in range(2):
                     nc.tensor.matmul_mx(
                         out=accs[h][:],
                         lhsT=xq[:, t, P * g : P * (g + 1)].bitcast(FP8X4),
@@ -196,91 +196,73 @@ def tile_hyplinear_kernel(tc, x, weight_words, weight_scales, bias, out):
 
         def chain_x(s, n):
             sl = slice(s, s + n)
-            G = nc.gpsimd
-            sxc = st.tile([P, n], F32, name="sxc%d" % n)
-            G.tensor_scalar_max(out=sxc[:], in0=sx_all[:, sl], scalar1=1e-15)
+            V = nc.vector
             xn = st.tile([P, n], F32, name="xn%d" % n)
-            nc.scalar.activation(out=xn[:], in_=sxc[:], func=AF.Sqrt)
-            nc.vector.reciprocal(out=rxn_all[:, sl], in_=xn[:])
+            nc.scalar.activation(out=xn[:], in_=sx_all[:, sl], func=AF.Sqrt, bias=1e-15)
+            uu = st.tile([P, n], F32, name="uu%d" % n)
+            V.tensor_scalar_min(out=uu[:], in0=xn[:], scalar1=1.0 - 1e-5)
+            V.reciprocal(out=rxn_all[:, sl], in_=xn[:])
             om = st.tile([P, n], F32, name="om%d" % n)
-            G.tensor_scalar(out=om[:], in0=xn[:], scalar1=1.0 - 1e-5, scalar2=-1.0, op0=AL.min, op1=AL.add)
+            nc.scalar.activation(out=om[:], in_=uu[:], func=AF.Identity, scale=-1.0, bias=1.0)
             rom = st.tile([P, n], F32, name="rom%d" % n)
-            nc.vector.reciprocal(out=rom[:], in_=om[:])
-            up = st.tile([P, n], F32, name="up%d" % n)
-            G.tensor_scalar(out=up[:], in0=om[:], scalar1=-1.0, scalar2=-2.0, op0=AL.mult, op1=AL.add)
-            G.tensor_tensor(out=w_all[:, sl], in0=up[:], in1=rom[:], op=AL.mult)
+            V.reciprocal(out=rom[:], in_=om[:])
+            V.scalar_tensor_tensor(out=w_all[:, sl], in0=uu[:], scalar=1.0, in1=rom[:], op0=AL.add, op1=AL.mult)
 
         def chain(s, n):
             sl = slice(s, s + n)
             V = nc.vector
-            G = nc.gpsimd
 
             def T(nm):
                 return st.tile([P, n], F32, name=nm)
 
-            sm = T("sm")
-            G.tensor_tensor(out=sm[:], in0=sq_all[:, sl, 0], in1=sq_all[:, sl, 1], op=AL.add)
             smc = T("smc")
-            G.tensor_scalar_max(out=smc[:], in0=sm[:], scalar1=1e-15)
+            V.scalar_tensor_tensor(out=smc[:], in0=sq_all[:, sl, 0], scalar=1e-15, in1=sq_all[:, sl, 1], op0=AL.max, op1=AL.add)
             mn = T("mn")
             nc.scalar.activation(out=mn[:], in_=smc[:], func=AF.Sqrt)
+            dd = T("dd")
+            V.tensor_tensor(out=dd[:], in0=d_all[:, sl, 0], in1=d_all[:, sl, 1], op=AL.add)
             qq = T("qq")
-            G.tensor_tensor(out=qq[:], in0=mn[:], in1=rxn_all[:, sl], op=AL.mult)
+            V.tensor_tensor(out=qq[:], in0=mn[:], in1=rxn_all[:, sl], op=AL.mult)
             ee = T("ee")
-            G.tensor_tensor(out=ee[:], in0=w_all[:, sl], in1=qq[:], op=AL.pow)
+            nc.gpsimd.tensor_tensor(out=ee[:], in0=w_all[:, sl], in1=qq[:], op=AL.pow)
             rmn = T("rmn")
             V.reciprocal(out=rmn[:], in_=mn[:])
             e1 = T("e1")
-            G.tensor_scalar(out=e1[:], in0=ee[:], scalar1=1e30, scalar2=1.0, op0=AL.min, op1=AL.add)
+            V.tensor_scalar(out=e1[:], in0=ee[:], scalar1=1e30, scalar2=1.0, op0=AL.min, op1=AL.add)
             re = T("re")
             V.reciprocal(out=re[:], in_=e1[:])
-            dd = T("dd")
-            G.tensor_tensor(out=dd[:], in0=d_all[:, sl, 0], in1=d_all[:, sl, 1], op=AL.add)
-            dh = T("dh")
-            G.tensor_scalar(out=dh[:], in0=dd[:], scalar1=h2[:], scalar2=0.0, op0=AL.mult, op1=AL.add)
             m2 = T("m2")
-            G.tensor_scalar(out=m2[:], in0=re[:], scalar1=(1.0 - MAXN) / 2.0, scalar2=-2.0, op0=AL.max, op1=AL.mult)
-            p1 = T("p1")
-            G.tensor_scalar_add(out=p1[:], in0=m2[:], scalar1=1.0)
-            c1 = T("c1")
-            G.tensor_tensor(out=c1[:], in0=p1[:], in1=rmn[:], op=AL.mult)
-            dx = T("dx")
-            G.tensor_tensor(out=dx[:], in0=dh[:], in1=c1[:], op=AL.mult)
-            p2 = T("p2")
-            G.tensor_scalar_add(out=p2[:], in0=m2[:], scalar1=2.0)
+            V.tensor_scalar(out=m2[:], in0=re[:], scalar1=(1.0 - MAXN) / 2.0, scalar2=-2.0, op0=AL.max, op1=AL.mult)
             nb = T("nb")
-            G.tensor_tensor(out=nb[:], in0=p2[:], in1=m2[:], op=AL.mult)
+            V.scalar_tensor_tensor(out=nb[:], in0=m2[:], scalar=2.0, in1=m2[:], op0=AL.add, op1=AL.mult)
+            c1 = T("c1")
+            V.scalar_tensor_tensor(out=c1[:], in0=m2[:], scalar=1.0, in1=rmn[:], op0=AL.add, op1=AL.mult)
             u1 = T("u1")
-            G.tensor_scalar(out=u1[:], in0=nb[:], scalar1=y2[:], scalar2=y2p1[:], op0=AL.mult, op1=AL.add)
+            nc.scalar.activation(out=u1[:], in_=nb[:], func=AF.Identity, scale=y2[:], bias=y2p1[:])
+            dx = T("dx")
+            V.scalar_tensor_tensor(out=dx[:], in0=dd[:], scalar=h2[:], in1=c1[:], op0=AL.mult, op1=AL.mult)
             den = T("den")
-            G.tensor_tensor(out=den[:], in0=u1[:], in1=dx[:], op=AL.add)
+            V.tensor_tensor(out=den[:], in0=u1[:], in1=dx[:], op=AL.add)
             rden = T("rden")
             V.reciprocal(out=rden[:], in_=den[:])
             nt = T("nt")
-            G.tensor_tensor(out=nt[:], in0=nb[:], in1=rden[:], op=AL.mult)
-            wv = T("wv")
-            G.tensor_scalar(out=wv[:], in0=nt[:], scalar1=k1c[:], scalar2=1.0 / C2 - 1.0, op0=AL.mult, op1=AL.add)
+            V.tensor_tensor(out=nt[:], in0=nb[:], in1=rden[:], op=AL.mult)
             wr = T("wr")
-            nc.scalar.activation(out=wr[:], in_=wv[:], func=AF.Relu)
+            nc.scalar.activation(out=wr[:], in_=nt[:], func=AF.Relu, scale=k1c[:], bias=1.0 / C2 - 1.0)
             sw = T("sw")
             nc.scalar.activation(out=sw[:], in_=wr[:], func=AF.Sqrt, bias=1.0)
+            a1 = T("a1")
+            nc.scalar.activation(out=a1[:], in_=nt[:], func=AF.Identity, scale=ny2[:], bias=1.0)
+            a2 = T("a2")
+            V.tensor_tensor(out=a2[:], in0=a1[:], in1=c1[:], op=AL.mult)
             rs = T("rs")
             V.reciprocal(out=rs[:], in_=sw[:])
-            a1 = T("a1")
-            G.tensor_scalar(out=a1[:], in0=nt[:], scalar1=ny2[:], scalar2=1.0, op0=AL.mult, op1=AL.add)
-            a2 = T("a2")
-            G.tensor_tensor(out=a2[:], in0=a1[:], in1=c1[:], op=AL.mult)
-            bh = T("bh")
-            G.tensor_scalar(out=bh[:], in0=nt[:], scalar1=nh[:], scalar2=0.0, op0=AL.mult, op1=AL.add)
-            G.tensor_tensor(out=b_all[:, sl], in0=bh[:], in1=rs[:], op=AL.mult)
-            G.tensor_tensor(out=a_all[:, sl], in0=a2[:], in1=rs[:], op=AL.mult)
+            V.tensor_tensor(out=a_all[:, sl], in0=a2[:], in1=rs[:], op=AL.mult)
+            V.scalar_tensor_tensor(out=b_all[:, sl], in0=nt[:], scalar=nh[:], in1=rs[:], op0=AL.mult, op1=AL.mult)
 
         def make_bb(t):
             bb = bb_pool.tile([P, N], F32, name="bb")
-            if t >= 20:
-                nc.scalar.activation(out=bb[:], in_=b_bc[:], func=AF.Copy, scale=b_all[:, t : t + 1])
-            else:
-                nc.gpsimd.tensor_scalar(out=bb[:], in0=b_bc[:], scalar1=b_all[:, t : t + 1], scalar2=0.0, op0=AL.mult, op1=AL.add)
+            nc.gpsimd.tensor_scalar(out=bb[:], in0=b_bc[:], scalar1=b_all[:, t : t + 1], scalar2=0.0, op0=AL.mult, op1=AL.add)
             return bb
 
         def stage_m2(t):

@@ -1,8 +1,6 @@
 from contextlib import ExitStack
 
-import concourse.bass as bass
 import concourse.mybir as mybir
-import concourse.tile as tile
 from concourse.masks import make_identity
 
 F32 = mybir.dt.float32
@@ -20,293 +18,265 @@ ROWS = 4096
 K = 1024
 N = 1024
 NT = ROWS // P
-HALF = 512
+PASSES = K // 512
+BANK = 512
 FLOPS = 2 * ROWS * K * N
 
-CHUNKS = [1, 1, 2, 4, 4, 4, 4, 4, 4, 4]
-GROUPS = [4] * 8
-XGROUPS = [4] * 8
-LX = 3
-M2_PER_STEP = 1
-M1_BANKS = 4
-M2_BANKS = 3
-LAG = 4
-MAXN = 0.996
-C2 = MAXN * MAXN
+MAX_NORM = 0.996
+MAX_NORM2 = MAX_NORM * MAX_NORM
+MIN_SQ = 1e-15
+
+X_LOADS = [1, 1, 2, 4, 4, 4, 4, 4, 4, 4]
+GROUP = 4
+LEAD = 3
+VECTOR_PAIRS = 6
 
 
 def tile_hyplinear_kernel(tc, x, weight_words, weight_scales, bias, out):
     nc = tc.nc
-    x_v = x.rearrange("(p t) k -> p t k", t=NT)
-    out_v = out.rearrange("(p t) n -> p t n", t=NT)
+    x_rows = x.rearrange("(p t) k -> p t k", t=NT)
+    out_rows = out.rearrange("(p t) n -> p t n", t=NT)
 
     with ExitStack() as ctx:
         keep = ctx.enter_context(tc.tile_pool(name="keep", bufs=1))
-        grp_pool = ctx.enter_context(tc.tile_pool(name="grp", bufs=3))
-        junk = ctx.enter_context(tc.tile_pool(name="junk", bufs=2))
-        st = ctx.enter_context(tc.tile_pool(name="st", bufs=3))
-        bb_pool = ctx.enter_context(tc.tile_pool(name="bb", bufs=3))
-        o_pool = ctx.enter_context(tc.tile_pool(name="o", bufs=4))
-        ps_t = ctx.enter_context(tc.psum_pool(name="ps_t", bufs=1))
-        ps_m = ctx.enter_context(tc.psum_pool(name="ps_m", bufs=M1_BANKS))
-        ps_o = ctx.enter_context(tc.psum_pool(name="ps_o", bufs=M2_BANKS))
+        grouped_pool = ctx.enter_context(tc.tile_pool(name="grouped", bufs=3))
+        unused = ctx.enter_context(tc.tile_pool(name="unused", bufs=2))
+        small = ctx.enter_context(tc.tile_pool(name="small", bufs=3))
+        bias_term_pool = ctx.enter_context(tc.tile_pool(name="bias_term", bufs=3))
+        out_pool = ctx.enter_context(tc.tile_pool(name="out_tile", bufs=4))
+        ps_transposed = ctx.enter_context(tc.psum_pool(name="ps_transposed", bufs=1))
+        ps_stats = ctx.enter_context(tc.psum_pool(name="ps_stats", bufs=4))
+        ps_out = ctx.enter_context(tc.psum_pool(name="ps_out", bufs=3))
 
-        wsc = keep.tile([P, 2, N], U8, align_bytes=64)
-        nc.vector.memset(wsc[:].bitcast(I32), 0)
-        halfc = keep.tile([P, 8], F32)
-        nc.vector.memset(halfc[:], 0.5)
-        mhalfc = keep.tile([P, 8], F32)
-        nc.vector.memset(mhalfc[:], -0.5)
-        ident = keep.tile([P, P], F32)
-        make_identity(nc, ident[:])
+        w_scales = keep.tile([P, PASSES, N], U8, align_bytes=64)
+        nc.vector.memset(w_scales[:].bitcast(I32), 0)
+        half = keep.tile([P, 1], F32)
+        nc.vector.memset(half[:], 0.5)
+        identity = keep.tile([P, P], F32)
+        make_identity(nc, identity[:])
 
-        xc = []
-        t0 = 0
-        tile_loc = []
-        for ci, cn in enumerate(CHUNKS):
-            xt_sb = keep.tile([P, cn, K], BF16, name="xc%d" % ci)
-            xc.append(xt_sb)
-            for k in range(cn):
-                tile_loc.append((ci, k))
-            t0 += cn
+        x_tiles = []
+        x_loads = []
+        for i, count in enumerate(X_LOADS):
+            loaded = keep.tile([P, count, K], BF16, name="x%d" % i)
+            x_loads.append((loaded, len(x_tiles), count))
+            for j in range(count):
+                x_tiles.append(loaded[:, j, :])
 
-        def load_chunk(ci):
-            s = sum(CHUNKS[:ci])
-            nc.sync.dma_start(out=xc[ci][:], in_=x_v[:, s : s + CHUNKS[ci], :])
+        def load_x(i):
+            loaded, first, count = x_loads[i]
+            nc.sync.dma_start(out=loaded[:], in_=x_rows[:, first : first + count, :])
 
-        load_chunk(0)
-        ws32 = weight_scales.bitcast(I32)
-        for q in range(4):
+        load_x(0)
+        scales32 = weight_scales.bitcast(I32)
+        for quadrant in range(4):
             nc.sync.dma_start(
-                out=wsc[32 * q : 32 * q + 4].bitcast(I32),
-                in_=ws32[:, 4 * q : 4 * q + 4, :].rearrange("g r n -> r g n"),
+                out=w_scales[32 * quadrant : 32 * quadrant + 4].bitcast(I32),
+                in_=scales32[:, 4 * quadrant : 4 * quadrant + 4, :].rearrange("g r n -> r g n"),
             )
-        wq = keep.tile([P, 2, 2 * N], U8, align_bytes=64)
-        nc.sync.dma_start(out=wq[:].bitcast(I32), in_=weight_words.bitcast(I32).rearrange("g p n -> p g n"))
-        b_bc = keep.tile([P, N], BF16)
-        nc.scalar.dma_start(out=b_bc[:], in_=bias.partition_broadcast(P))
-        for ci in range(1, len(CHUNKS)):
-            load_chunk(ci)
+        w_codes = keep.tile([P, PASSES, 2 * N], U8, align_bytes=64)
+        nc.sync.dma_start(out=w_codes[:].bitcast(I32), in_=weight_words.bitcast(I32).rearrange("g p n -> p g n"))
+        bias_all = keep.tile([P, N], BF16)
+        nc.scalar.dma_start(out=bias_all[:], in_=bias.partition_broadcast(P))
+        for i in range(1, len(X_LOADS)):
+            load_x(i)
 
-        xq = keep.tile([P, NT, 256], U32, align_bytes=64)
-        xs = keep.tile([P, NT, 256], U8, align_bytes=64)
-        sx_all = keep.tile([P, NT], F32)
-        sq_all = keep.tile([P, NT, 2], F32)
-        d_all = keep.tile([P, NT, 2], F32)
-        a_all = keep.tile([P, NT], F32)
-        b_all = keep.tile([P, NT], F32)
-        rxn_all = keep.tile([P, NT], F32)
-        w_all = keep.tile([P, NT], F32)
+        x_codes = keep.tile([P, NT, PASSES * P], U32, align_bytes=64)
+        x_scales = keep.tile([P, NT, PASSES * P], U8, align_bytes=64)
+        sx = keep.tile([P, NT], F32)
+        sm = keep.tile([P, NT, 2], F32)
+        d = keep.tile([P, NT, 2], F32)
+        coef_mx = keep.tile([P, NT], F32)
+        coef_bias = keep.tile([P, NT], F32)
+        inv_xn = keep.tile([P, NT], F32)
+        ratio = keep.tile([P, NT], F32)
 
-        jb = junk.tile([P, N], BF16, name="jx")
-        sb = keep.tile([P, 1], F32)
-        nc.scalar.activation(out=jb[:], in_=b_bc[:], func=AF.Square, accum_out=sb[:])
-        sbc = keep.tile([P, 1], F32)
-        nc.vector.tensor_scalar_max(out=sbc[:], in0=sb[:], scalar1=1e-15)
-        bn = keep.tile([P, 1], F32)
-        nc.gpsimd.tensor_tensor(out=bn[:], in0=sbc[:], in1=halfc[:, 0:1], op=AL.pow)
-        tb = keep.tile([P, 1], F32)
-        nc.scalar.activation(out=tb[:], in_=bn[:], func=AF.Tanh)
-        rbn = keep.tile([P, 1], F32)
-        nc.vector.reciprocal(out=rbn[:], in_=bn[:])
-        hh = keep.tile([P, 1], F32)
-        nc.vector.scalar_tensor_tensor(out=hh[:], in0=tb[:], scalar=MAXN, in1=rbn[:], op0=AL.min, op1=AL.mult)
-        h2 = keep.tile([P, 1], F32)
-        nc.vector.tensor_scalar_mul(out=h2[:], in0=hh[:], scalar1=2.0)
-        nh = keep.tile([P, 1], F32)
-        nc.vector.tensor_scalar_mul(out=nh[:], in0=hh[:], scalar1=-1.0)
-        hsq = keep.tile([P, 1], F32)
-        nc.vector.tensor_tensor(out=hsq[:], in0=hh[:], in1=hh[:], op=AL.mult)
-        y2 = keep.tile([P, 1], F32)
-        nc.vector.tensor_tensor(out=y2[:], in0=hsq[:], in1=sb[:], op=AL.mult)
-        ny2 = keep.tile([P, 1], F32)
-        nc.vector.tensor_scalar_mul(out=ny2[:], in0=y2[:], scalar1=-1.0)
-        y2p1 = keep.tile([P, 1], F32)
-        nc.vector.tensor_scalar_add(out=y2p1[:], in0=y2[:], scalar1=1.0)
-        k1c = keep.tile([P, 1], F32)
-        nc.vector.tensor_scalar(out=k1c[:], in0=y2[:], scalar1=-1.0 / C2, scalar2=1.0 / C2, op0=AL.mult, op1=AL.add)
+        def const(name):
+            return keep.tile([P, 1], F32, name=name)
 
-        def stage_x(s):
-            grp = grp_pool.tile([P, 2, K], BF16, name="grp", align_bytes=64)
-            xts = []
+        V = nc.vector
+        squares = unused.tile([P, N], BF16, name="x_squares")
+        sb = const("sb")
+        nc.scalar.activation(out=squares[:], in_=bias_all[:], func=AF.Square, accum_out=sb[:])
+        sb_floor = const("sb_floor")
+        V.tensor_scalar_max(out=sb_floor[:], in0=sb[:], scalar1=MIN_SQ)
+        bias_norm = const("bias_norm")
+        nc.gpsimd.tensor_tensor(out=bias_norm[:], in0=sb_floor[:], in1=half[:], op=AL.pow)
+        bias_tanh = const("bias_tanh")
+        nc.scalar.activation(out=bias_tanh[:], in_=bias_norm[:], func=AF.Tanh)
+        inv_bias_norm = const("inv_bias_norm")
+        V.reciprocal(out=inv_bias_norm[:], in_=bias_norm[:])
+        h = const("h")
+        V.scalar_tensor_tensor(out=h[:], in0=bias_tanh[:], scalar=MAX_NORM, in1=inv_bias_norm[:], op0=AL.min, op1=AL.mult)
+        two_h = const("two_h")
+        V.tensor_scalar_mul(out=two_h[:], in0=h[:], scalar1=2.0)
+        minus_h = const("minus_h")
+        V.tensor_scalar_mul(out=minus_h[:], in0=h[:], scalar1=-1.0)
+        h_sq = const("h_sq")
+        V.tensor_tensor(out=h_sq[:], in0=h[:], in1=h[:], op=AL.mult)
+        y2 = const("y2")
+        V.tensor_tensor(out=y2[:], in0=h_sq[:], in1=sb[:], op=AL.mult)
+        minus_y2 = const("minus_y2")
+        V.tensor_scalar_mul(out=minus_y2[:], in0=y2[:], scalar1=-1.0)
+        one_plus_y2 = const("one_plus_y2")
+        V.tensor_scalar_add(out=one_plus_y2[:], in0=y2[:], scalar1=1.0)
+        clamp_slope = const("clamp_slope")
+        V.tensor_scalar(out=clamp_slope[:], in0=y2[:], scalar1=-1.0 / MAX_NORM2, scalar2=1.0 / MAX_NORM2, op0=AL.mult, op1=AL.add)
+
+        def transpose_pair(pair):
+            grouped = grouped_pool.tile([P, 2, K], BF16, name="grouped", align_bytes=64)
+            transposed = []
             for j in range(2):
-                ci, k = tile_loc[2 * s + j]
-                xw = xc[ci][:, k, :].bitcast(F32)
-                xt = ps_t.tile([P, 4, P], F32, name="xt")
-                xts.append(xt)
-                for g in range(2):
+                words = x_tiles[2 * pair + j].bitcast(F32)
+                bank = ps_transposed.tile([P, 2 * PASSES, P], F32, name="transposed")
+                transposed.append(bank)
+                for g in range(PASSES):
                     for u in range(2):
-                        nc.tensor.transpose(xt[:, 2 * g + u, :], xw[:, 256 * g + u : 256 * (g + 1) : 2], ident[:])
+                        nc.tensor.transpose(bank[:, 2 * g + u, :], words[:, 256 * g + u : 256 * (g + 1) : 2], identity[:])
             for j in range(2):
-                dst = grp[:, j, :].bitcast(F32).rearrange("p (g r u) -> p g r u", g=2, u=2)
-                src = xts[j][:].rearrange("p (g u) r -> p g r u", g=2)
-                if s < 6:
+                dst = grouped[:, j, :].bitcast(F32).rearrange("p (g r u) -> p g r u", g=PASSES, u=2)
+                src = transposed[j][:].rearrange("p (g u) r -> p g r u", g=PASSES)
+                if pair < VECTOR_PAIRS:
                     nc.vector.tensor_copy(out=dst, in_=src)
                 else:
                     nc.scalar.copy(out=dst, in_=src)
-            return grp
+            return grouped
 
-        def quant(s, grp):
+        def quantise_pair(pair, grouped):
+            tiles = slice(2 * pair, 2 * pair + 2)
             nc.vector.quantize_mx(
-                out=xq[:, 2 * s : 2 * s + 2, :].rearrange("p a c -> p (a c)").bitcast(FP8X4),
-                scales=xs[:, 2 * s : 2 * s + 2, :].rearrange("p a c -> p (a c)"),
-                in_=grp[:].rearrange("p a c -> p (a c)"),
+                out=x_codes[:, tiles, :].rearrange("p a c -> p (a c)").bitcast(FP8X4),
+                scales=x_scales[:, tiles, :].rearrange("p a c -> p (a c)"),
+                in_=grouped[:].rearrange("p a c -> p (a c)"),
             )
 
-        def xnorm(t):
-            ci, k = tile_loc[t]
-            jx = junk.tile([P, K], BF16, name="jx")
-            nc.scalar.activation(out=jx[:], in_=xc[ci][:, k, :], func=AF.Square, accum_out=sx_all[:, t : t + 1])
+        def x_norm(t):
+            squares = unused.tile([P, K], BF16, name="x_squares")
+            nc.scalar.activation(out=squares[:], in_=x_tiles[t], func=AF.Square, accum_out=sx[:, t : t + 1])
 
-        def mm(t, pool):
-            accs = []
-            for h in range(2):
-                acc = pool.tile([P, HALF], F32, name="acc")
-                accs.append(acc)
-            for h in range(2):
-                for g in range(2):
+        def product(t, pool):
+            banks = []
+            for half_n in range(2):
+                banks.append(pool.tile([P, BANK], F32, name="mx"))
+            for half_n in range(2):
+                for g in range(PASSES):
                     nc.tensor.matmul_mx(
-                        out=accs[h][:],
-                        lhsT=xq[:, t, P * g : P * (g + 1)].bitcast(FP8X4),
-                        lhsT_scale=xs[:, t, P * g : P * (g + 1)],
-                        rhs=wq[:, g, 2 * HALF * h : 2 * HALF * (h + 1)].bitcast(FP4X4),
-                        rhs_scale=wsc[:, g, HALF * h : HALF * (h + 1)],
+                        out=banks[half_n][:],
+                        lhsT=x_codes[:, t, P * g : P * (g + 1)].bitcast(FP8X4),
+                        lhsT_scale=x_scales[:, t, P * g : P * (g + 1)],
+                        rhs=w_codes[:, g, 2 * BANK * half_n : 2 * BANK * (half_n + 1)].bitcast(FP4X4),
+                        rhs_scale=w_scales[:, g, BANK * half_n : BANK * (half_n + 1)],
                         start=(g == 0),
-                        stop=(g == 1),
+                        stop=(g == PASSES - 1),
                     )
-            return accs
+            return banks
 
-        def sq(t, h, acc):
-            js = junk.tile([P, HALF], BF16, name="js")
-            nc.scalar.activation(out=js[:], in_=acc[:], func=AF.Square, accum_out=sq_all[:, t, h : h + 1])
-
-        def dot(t, h, acc):
-            jv = junk.tile([P, HALF], F32, name="jv")
-            nc.vector.scalar_tensor_tensor(
-                out=jv[:], in0=acc[:], scalar=1.0, in1=b_bc[:, HALF * h : HALF * (h + 1)],
-                op0=AL.mult, op1=AL.mult, accum_out=d_all[:, t, h : h + 1],
-            )
-
-        def stage_m1(t):
-            accs = mm(t, ps_m)
-            sq(t, 0, accs[0])
-            dot(t, 1, accs[1])
-            sq(t, 1, accs[1])
-            dot(t, 0, accs[0])
-
-        def chain_x(s, n):
-            sl = slice(s, s + n)
-            V = nc.vector
-            xn = st.tile([P, n], F32, name="xn%d" % n)
-            nc.scalar.activation(out=xn[:], in_=sx_all[:, sl], func=AF.Sqrt, bias=1e-15)
-            uu = st.tile([P, n], F32, name="uu%d" % n)
-            V.tensor_scalar_min(out=uu[:], in0=xn[:], scalar1=1.0 - 1e-5)
-            V.reciprocal(out=rxn_all[:, sl], in_=xn[:])
-            om = st.tile([P, n], F32, name="om%d" % n)
-            nc.scalar.activation(out=om[:], in_=uu[:], func=AF.Identity, scale=-1.0, bias=1.0)
-            rom = st.tile([P, n], F32, name="rom%d" % n)
-            V.reciprocal(out=rom[:], in_=om[:])
-            V.scalar_tensor_tensor(out=w_all[:, sl], in0=uu[:], scalar=1.0, in1=rom[:], op0=AL.add, op1=AL.mult)
-
-        def chain(s, n):
-            sl = slice(s, s + n)
-            V = nc.vector
-
-            def T(nm):
-                return st.tile([P, n], F32, name=nm)
-
-            smc = T("smc")
-            V.scalar_tensor_tensor(out=smc[:], in0=sq_all[:, sl, 0], scalar=1e-15, in1=sq_all[:, sl, 1], op0=AL.max, op1=AL.add)
-            mn = T("mn")
-            nc.scalar.activation(out=mn[:], in_=smc[:], func=AF.Sqrt)
-            dd = T("dd")
-            V.tensor_tensor(out=dd[:], in0=d_all[:, sl, 0], in1=d_all[:, sl, 1], op=AL.add)
-            qq = T("qq")
-            V.tensor_tensor(out=qq[:], in0=mn[:], in1=rxn_all[:, sl], op=AL.mult)
-            ee = T("ee")
-            nc.gpsimd.tensor_tensor(out=ee[:], in0=w_all[:, sl], in1=qq[:], op=AL.pow)
-            rmn = T("rmn")
-            V.reciprocal(out=rmn[:], in_=mn[:])
-            e1 = T("e1")
-            V.tensor_scalar(out=e1[:], in0=ee[:], scalar1=1e30, scalar2=1.0, op0=AL.min, op1=AL.add)
-            re = T("re")
-            V.reciprocal(out=re[:], in_=e1[:])
-            m2 = T("m2")
-            V.tensor_scalar(out=m2[:], in0=re[:], scalar1=(1.0 - MAXN) / 2.0, scalar2=-2.0, op0=AL.max, op1=AL.mult)
-            nb = T("nb")
-            V.scalar_tensor_tensor(out=nb[:], in0=m2[:], scalar=2.0, in1=m2[:], op0=AL.add, op1=AL.mult)
-            c1 = T("c1")
-            V.scalar_tensor_tensor(out=c1[:], in0=m2[:], scalar=1.0, in1=rmn[:], op0=AL.add, op1=AL.mult)
-            u1 = T("u1")
-            nc.scalar.activation(out=u1[:], in_=nb[:], func=AF.Identity, scale=y2[:], bias=y2p1[:])
-            dx = T("dx")
-            V.scalar_tensor_tensor(out=dx[:], in0=dd[:], scalar=h2[:], in1=c1[:], op0=AL.mult, op1=AL.mult)
-            den = T("den")
-            V.tensor_tensor(out=den[:], in0=u1[:], in1=dx[:], op=AL.add)
-            rden = T("rden")
-            V.reciprocal(out=rden[:], in_=den[:])
-            nt = T("nt")
-            V.tensor_tensor(out=nt[:], in0=nb[:], in1=rden[:], op=AL.mult)
-            wr = T("wr")
-            nc.scalar.activation(out=wr[:], in_=nt[:], func=AF.Relu, scale=k1c[:], bias=1.0 / C2 - 1.0)
-            sw = T("sw")
-            nc.scalar.activation(out=sw[:], in_=wr[:], func=AF.Sqrt, bias=1.0)
-            a1 = T("a1")
-            nc.scalar.activation(out=a1[:], in_=nt[:], func=AF.Identity, scale=ny2[:], bias=1.0)
-            a2 = T("a2")
-            V.tensor_tensor(out=a2[:], in0=a1[:], in1=c1[:], op=AL.mult)
-            rs = T("rs")
-            V.reciprocal(out=rs[:], in_=sw[:])
-            V.tensor_tensor(out=a_all[:, sl], in0=a2[:], in1=rs[:], op=AL.mult)
-            V.scalar_tensor_tensor(out=b_all[:, sl], in0=nt[:], scalar=nh[:], in1=rs[:], op0=AL.mult, op1=AL.mult)
-
-        def make_bb(t):
-            bb = bb_pool.tile([P, N], F32, name="bb")
-            nc.gpsimd.tensor_scalar(out=bb[:], in0=b_bc[:], scalar1=b_all[:, t : t + 1], scalar2=0.0, op0=AL.mult, op1=AL.add)
-            return bb
-
-        def stage_m2(t):
-            bb = make_bb(t)
-            accs = mm(t, ps_o)
-            o = o_pool.tile([P, N], F32, name="o")
-            for h in range(2):
-                hs = slice(HALF * h, HALF * (h + 1))
+        def statistics_sweep(t):
+            banks = product(t, ps_stats)
+            for half_n in range(2):
+                products = unused.tile([P, BANK], F32, name="products")
                 nc.vector.scalar_tensor_tensor(
-                    out=o[:, hs], in0=accs[h][:], scalar=a_all[:, t : t + 1], in1=bb[:, hs], op0=AL.mult, op1=AL.add
+                    out=products[:], in0=banks[half_n][:], scalar=1.0, in1=bias_all[:, BANK * half_n : BANK * (half_n + 1)],
+                    op0=AL.mult, op1=AL.mult, accum_out=d[:, t, half_n : half_n + 1],
                 )
-            nc.sync.dma_start(out=out_v[:, t, :], in_=o[:])
+                squares = unused.tile([P, BANK], BF16, name="mx_squares")
+                nc.scalar.activation(out=squares[:], in_=banks[half_n][:], func=AF.Square, accum_out=sm[:, t, half_n : half_n + 1])
 
-        last_of_group = {}
-        g0 = 0
-        for gn in GROUPS:
-            last_of_group[g0 + gn - 1] = (g0, gn)
-            g0 += gn
-        last_of_xgroup = {}
-        g0 = 0
-        for gn in XGROUPS:
-            last_of_xgroup[g0 + gn - 1] = (g0, gn)
-            g0 += gn
-        ready = 0
-        done2 = 0
-        i = 0
-        grp = None
-        while done2 < NT:
-            a = i - LX
-            if i % 2 == 0 and i < NT:
-                grp = stage_x(i // 2)
-            if i < NT:
-                xnorm(i)
-            if i in last_of_xgroup:
-                chain_x(last_of_xgroup[i][0], last_of_xgroup[i][1])
-            if 0 <= a < NT:
-                stage_m1(a)
-            for q in range(M2_PER_STEP):
-                if done2 < ready:
-                    stage_m2(done2)
-                    done2 += 1
-            if i % 2 == 0 and i < NT:
-                quant(i // 2, grp)
-            if a in last_of_group:
-                chain(last_of_group[a][0], last_of_group[a][1])
-                ready = a + 1
-            i += 1
+        def tmp(name):
+            return small.tile([P, GROUP], F32, name=name)
+
+        def x_scalars(first):
+            g = slice(first, first + GROUP)
+            xn = tmp("xn")
+            nc.scalar.activation(out=xn[:], in_=sx[:, g], func=AF.Sqrt, bias=MIN_SQ)
+            u = tmp("u")
+            V.tensor_scalar_min(out=u[:], in0=xn[:], scalar1=1.0 - 1e-5)
+            V.reciprocal(out=inv_xn[:, g], in_=xn[:])
+            one_minus_u = tmp("one_minus_u")
+            nc.scalar.activation(out=one_minus_u[:], in_=u[:], func=AF.Identity, scale=-1.0, bias=1.0)
+            inv_one_minus_u = tmp("inv_one_minus_u")
+            V.reciprocal(out=inv_one_minus_u[:], in_=one_minus_u[:])
+            V.scalar_tensor_tensor(out=ratio[:, g], in0=u[:], scalar=1.0, in1=inv_one_minus_u[:], op0=AL.add, op1=AL.mult)
+
+        def row_scalars(first):
+            g = slice(first, first + GROUP)
+            sm_floor = tmp("sm_floor")
+            V.scalar_tensor_tensor(out=sm_floor[:], in0=sm[:, g, 0], scalar=MIN_SQ, in1=sm[:, g, 1], op0=AL.max, op1=AL.add)
+            mn = tmp("mn")
+            nc.scalar.activation(out=mn[:], in_=sm_floor[:], func=AF.Sqrt)
+            d_sum = tmp("d_sum")
+            V.tensor_tensor(out=d_sum[:], in0=d[:, g, 0], in1=d[:, g, 1], op=AL.add)
+            exponent = tmp("exponent")
+            V.tensor_tensor(out=exponent[:], in0=mn[:], in1=inv_xn[:, g], op=AL.mult)
+            e_pow = tmp("e_pow")
+            nc.gpsimd.tensor_tensor(out=e_pow[:], in0=ratio[:, g], in1=exponent[:], op=AL.pow)
+            inv_mn = tmp("inv_mn")
+            V.reciprocal(out=inv_mn[:], in_=mn[:])
+            e_plus_1 = tmp("e_plus_1")
+            V.tensor_scalar(out=e_plus_1[:], in0=e_pow[:], scalar1=1e30, scalar2=1.0, op0=AL.min, op1=AL.add)
+            inv_e = tmp("inv_e")
+            V.reciprocal(out=inv_e[:], in_=e_plus_1[:])
+            rho_minus_1 = tmp("rho_minus_1")
+            V.tensor_scalar(out=rho_minus_1[:], in0=inv_e[:], scalar1=(1.0 - MAX_NORM) / 2.0, scalar2=-2.0, op0=AL.max, op1=AL.mult)
+            minus_beta = tmp("minus_beta")
+            V.scalar_tensor_tensor(out=minus_beta[:], in0=rho_minus_1[:], scalar=2.0, in1=rho_minus_1[:], op0=AL.add, op1=AL.mult)
+            res_scale = tmp("res_scale")
+            V.scalar_tensor_tensor(out=res_scale[:], in0=rho_minus_1[:], scalar=1.0, in1=inv_mn[:], op0=AL.add, op1=AL.mult)
+            den_part = tmp("den_part")
+            nc.scalar.activation(out=den_part[:], in_=minus_beta[:], func=AF.Identity, scale=y2[:], bias=one_plus_y2[:])
+            two_xy = tmp("two_xy")
+            V.scalar_tensor_tensor(out=two_xy[:], in0=d_sum[:], scalar=two_h[:], in1=res_scale[:], op0=AL.mult, op1=AL.mult)
+            den = tmp("den")
+            V.tensor_tensor(out=den[:], in0=den_part[:], in1=two_xy[:], op=AL.add)
+            inv_den = tmp("inv_den")
+            V.reciprocal(out=inv_den[:], in_=den[:])
+            minus_tau = tmp("minus_tau")
+            V.tensor_tensor(out=minus_tau[:], in0=minus_beta[:], in1=inv_den[:], op=AL.mult)
+            excess = tmp("excess")
+            nc.scalar.activation(out=excess[:], in_=minus_tau[:], func=AF.Relu, scale=clamp_slope[:], bias=1.0 / MAX_NORM2 - 1.0)
+            shrink = tmp("shrink")
+            nc.scalar.activation(out=shrink[:], in_=excess[:], func=AF.Sqrt, bias=1.0)
+            alpha_over_den = tmp("alpha_over_den")
+            nc.scalar.activation(out=alpha_over_den[:], in_=minus_tau[:], func=AF.Identity, scale=minus_y2[:], bias=1.0)
+            unclamped_a = tmp("unclamped_a")
+            V.tensor_tensor(out=unclamped_a[:], in0=alpha_over_den[:], in1=res_scale[:], op=AL.mult)
+            inv_shrink = tmp("inv_shrink")
+            V.reciprocal(out=inv_shrink[:], in_=shrink[:])
+            V.tensor_tensor(out=coef_mx[:, g], in0=unclamped_a[:], in1=inv_shrink[:], op=AL.mult)
+            V.scalar_tensor_tensor(out=coef_bias[:, g], in0=minus_tau[:], scalar=minus_h[:], in1=inv_shrink[:], op0=AL.mult, op1=AL.mult)
+
+        def output_sweep(t):
+            bias_term = bias_term_pool.tile([P, N], F32, name="bias_term")
+            nc.gpsimd.tensor_scalar(out=bias_term[:], in0=bias_all[:], scalar1=coef_bias[:, t : t + 1], scalar2=0.0, op0=AL.mult, op1=AL.add)
+            banks = product(t, ps_out)
+            out_tile = out_pool.tile([P, N], F32, name="out_tile")
+            for half_n in range(2):
+                cols = slice(BANK * half_n, BANK * (half_n + 1))
+                nc.vector.scalar_tensor_tensor(
+                    out=out_tile[:, cols], in0=banks[half_n][:], scalar=coef_mx[:, t : t + 1], in1=bias_term[:, cols], op0=AL.mult, op1=AL.add
+                )
+            nc.sync.dma_start(out=out_rows[:, t, :], in_=out_tile[:])
+
+        with_scalars = 0
+        finished = 0
+        step = 0
+        grouped = None
+        while finished < NT:
+            stats_tile = step - LEAD
+            if step % 2 == 0 and step < NT:
+                grouped = transpose_pair(step // 2)
+            if step < NT:
+                x_norm(step)
+                if step % GROUP == GROUP - 1:
+                    x_scalars(step - GROUP + 1)
+            if 0 <= stats_tile < NT:
+                statistics_sweep(stats_tile)
+            if finished < with_scalars:
+                output_sweep(finished)
+                finished += 1
+            if step % 2 == 0 and step < NT:
+                quantise_pair(step // 2, grouped)
+            if 0 <= stats_tile < NT and stats_tile % GROUP == GROUP - 1:
+                row_scalars(stats_tile - GROUP + 1)
+                with_scalars = stats_tile + 1
+            step += 1

@@ -76,10 +76,20 @@ def tile_hyplinear_kernel(tc, x, weight_words, weight_scales, bias, out):
             )
         w_codes = keep.tile([P, PASSES, 2 * N], U8, align_bytes=64)
         nc.sync.dma_start(out=w_codes[:].bitcast(I32), in_=weight_words.bitcast(I32).rearrange("g p n -> p g n"))
-        bias_all = keep.tile([P, N], BF16)
-        nc.scalar.dma_start(out=bias_all[:], in_=bias.partition_broadcast(P))
+        bias_row = keep.tile([P, N], BF16)
+        nc.vector.memset(bias_row[:], 0.0)
+        nc.scalar.dma_start(out=bias_row[0:1, :], in_=bias.rearrange("(o n) -> o n", o=1))
         for i in range(1, len(X_LOADS)):
             load_x(i)
+
+        ones = keep.tile([P, P], BF16)
+        nc.vector.memset(ones[:], 1.0)
+        bias_all = keep.tile([P, N], BF16)
+        for half_n in range(2):
+            cols = slice(BANK * half_n, BANK * (half_n + 1))
+            spread = ps_stats.tile([P, BANK], F32, name="mx")
+            nc.tensor.matmul(out=spread[:], lhsT=ones[:], rhs=bias_row[:, cols], start=True, stop=True)
+            nc.vector.tensor_copy(out=bias_all[:, cols], in_=spread[:])
 
         x_codes = keep.tile([P, NT, PASSES * P], U32, align_bytes=64)
         x_scales = keep.tile([P, NT, PASSES * P], U8, align_bytes=64)
@@ -173,14 +183,22 @@ def tile_hyplinear_kernel(tc, x, weight_words, weight_scales, bias, out):
 
         def statistics_sweep(t):
             banks = product(t, ps_stats)
-            for half_n in range(2):
+
+            def sum_of_squares(half_n):
+                squares = unused.tile([P, BANK], BF16, name="mx_squares")
+                nc.scalar.activation(out=squares[:], in_=banks[half_n][:], func=AF.Square, accum_out=sm[:, t, half_n : half_n + 1])
+
+            def dot_with_bias(half_n):
                 products = unused.tile([P, BANK], F32, name="products")
                 nc.vector.scalar_tensor_tensor(
                     out=products[:], in0=banks[half_n][:], scalar=1.0, in1=bias_all[:, BANK * half_n : BANK * (half_n + 1)],
                     op0=AL.mult, op1=AL.mult, accum_out=d[:, t, half_n : half_n + 1],
                 )
-                squares = unused.tile([P, BANK], BF16, name="mx_squares")
-                nc.scalar.activation(out=squares[:], in_=banks[half_n][:], func=AF.Square, accum_out=sm[:, t, half_n : half_n + 1])
+
+            sum_of_squares(0)
+            dot_with_bias(1)
+            sum_of_squares(1)
+            dot_with_bias(0)
 
         def tmp(name):
             return small.tile([P, GROUP], F32, name=name)

@@ -1,3 +1,4 @@
+import math
 from contextlib import ExitStack
 
 import concourse.mybir as mybir
@@ -25,11 +26,16 @@ FLOPS = 2 * ROWS * K * N
 MAX_NORM = 0.996
 MAX_NORM2 = MAX_NORM * MAX_NORM
 MIN_SQ = 1e-15
+MAX_E = 2.0 / (1.0 - MAX_NORM) - 1.0
 
 X_LOADS = [1, 1, 2, 4, 4, 4, 4, 4, 4, 4]
-GROUP = 4
-LEAD = 3
-VECTOR_PAIRS = 6
+GROUPS = [4, 4, 4, 4, 4, 4, 4, 2, 2]
+SLOTS = 5
+CHAIN_STEPS = 3
+LAG = max(GROUPS) + CHAIN_STEPS
+DRAIN = NT - LAG
+SQUARES_LEAD = 4
+VECTOR_COPIES = 8
 
 
 def tile_hyplinear_kernel(tc, x, weight_words, weight_scales, bias, out):
@@ -41,19 +47,29 @@ def tile_hyplinear_kernel(tc, x, weight_words, weight_scales, bias, out):
         keep = ctx.enter_context(tc.tile_pool(name="keep", bufs=1))
         grouped_pool = ctx.enter_context(tc.tile_pool(name="grouped", bufs=3))
         unused = ctx.enter_context(tc.tile_pool(name="unused", bufs=2))
-        small = ctx.enter_context(tc.tile_pool(name="small", bufs=3))
-        bias_term_pool = ctx.enter_context(tc.tile_pool(name="bias_term", bufs=3))
+        bias_term_pool = ctx.enter_context(tc.tile_pool(name="bias_term", bufs=2))
         out_pool = ctx.enter_context(tc.tile_pool(name="out_tile", bufs=4))
         ps_transposed = ctx.enter_context(tc.psum_pool(name="ps_transposed", bufs=1))
         ps_stats = ctx.enter_context(tc.psum_pool(name="ps_stats", bufs=4))
         ps_out = ctx.enter_context(tc.psum_pool(name="ps_out", bufs=3))
+        ctx.enter_context(tc.manual_schedule())
+        V = nc.vector
 
-        w_scales = keep.tile([P, PASSES, N], U8, align_bytes=64)
-        nc.vector.memset(w_scales[:].bitcast(I32), 0)
-        half = keep.tile([P, 1], F32)
-        nc.vector.memset(half[:], 0.5)
+        warm = keep.tile([P, 1], F32)
+        V.memset(warm[:], 1.0)
+        nc.scalar.activation(out=warm[:], in_=warm[:], func=AF.Abs_reciprocal_sqrt)
         identity = keep.tile([P, P], F32)
         make_identity(nc, identity[:])
+        w_scales = keep.tile([P, PASSES, N], U8, align_bytes=64)
+        V.memset(w_scales[:].bitcast(I32), 0)
+        bias_row = keep.tile([P, N], BF16)
+        V.memset(bias_row[:], 0.0)
+        ones = keep.tile([P, P], BF16)
+        V.memset(ones[:], 1.0)
+        zero = keep.tile([P, 1], F32)
+        V.memset(zero[:], 0.0)
+        half = keep.tile([P, 1], F32)
+        V.memset(half[:], 0.5)
 
         x_tiles = []
         x_loads = []
@@ -74,91 +90,185 @@ def tile_hyplinear_kernel(tc, x, weight_words, weight_scales, bias, out):
                 out=w_scales[32 * quadrant : 32 * quadrant + 4].bitcast(I32),
                 in_=scales32[:, 4 * quadrant : 4 * quadrant + 4, :].rearrange("g r n -> r g n"),
             )
+        load_x(1)
         w_codes = keep.tile([P, PASSES, 2 * N], U8, align_bytes=64)
         nc.sync.dma_start(out=w_codes[:].bitcast(I32), in_=weight_words.bitcast(I32).rearrange("g p n -> p g n"))
-        bias_row = keep.tile([P, N], BF16)
-        nc.vector.memset(bias_row[:], 0.0)
-        nc.scalar.dma_start(out=bias_row[0:1, :], in_=bias.rearrange("(o n) -> o n", o=1))
-        for i in range(1, len(X_LOADS)):
+        nc.sync.dma_start(out=bias_row[0:1, :], in_=bias.rearrange("(o n) -> o n", o=1))
+        for i in range(2, len(X_LOADS)):
             load_x(i)
 
-        ones = keep.tile([P, P], BF16)
-        nc.vector.memset(ones[:], 1.0)
         bias_all = keep.tile([P, N], BF16)
-        for half_n in range(2):
-            cols = slice(BANK * half_n, BANK * (half_n + 1))
-            spread = ps_stats.tile([P, BANK], F32, name="mx")
-            nc.tensor.matmul(out=spread[:], lhsT=ones[:], rhs=bias_row[:, cols], start=True, stop=True)
-            nc.vector.tensor_copy(out=bias_all[:, cols], in_=spread[:])
-
         x_codes = keep.tile([P, NT, PASSES * P], U32, align_bytes=64)
         x_scales = keep.tile([P, NT, PASSES * P], U8, align_bytes=64)
         sx = keep.tile([P, NT], F32)
-        sm = keep.tile([P, NT, 2], F32)
-        d = keep.tile([P, NT, 2], F32)
+        parts = keep.tile([P, 2, NT, 2], F32)
+        sums = keep.tile([P, 2, NT], F32)
         coef_mx = keep.tile([P, NT], F32)
         coef_bias = keep.tile([P, NT], F32)
+        full_coef_bias = keep.tile([P, NT], F32)
         inv_xn = keep.tile([P, NT], F32)
         ratio = keep.tile([P, NT], F32)
+
+        waiting = {}
+
+        def put(place, call):
+            waiting.setdefault(place, []).append(call)
+
+        def run_place(place):
+            for call in waiting.get(place, []):
+                call()
 
         def const(name):
             return keep.tile([P, 1], F32, name=name)
 
-        V = nc.vector
-        squares = unused.tile([P, N], BF16, name="x_squares")
-        sb = const("sb")
-        nc.scalar.activation(out=squares[:], in_=bias_all[:], func=AF.Square, accum_out=sb[:])
-        sb_floor = const("sb_floor")
-        V.tensor_scalar_max(out=sb_floor[:], in0=sb[:], scalar1=MIN_SQ)
-        bias_norm = const("bias_norm")
-        nc.gpsimd.tensor_tensor(out=bias_norm[:], in0=sb_floor[:], in1=half[:], op=AL.pow)
-        bias_tanh = const("bias_tanh")
-        nc.scalar.activation(out=bias_tanh[:], in_=bias_norm[:], func=AF.Tanh)
-        inv_bias_norm = const("inv_bias_norm")
-        V.reciprocal(out=inv_bias_norm[:], in_=bias_norm[:])
-        h = const("h")
-        V.scalar_tensor_tensor(out=h[:], in0=bias_tanh[:], scalar=MAX_NORM, in1=inv_bias_norm[:], op0=AL.min, op1=AL.mult)
-        two_h = const("two_h")
-        V.tensor_scalar_mul(out=two_h[:], in0=h[:], scalar1=2.0)
-        minus_h = const("minus_h")
-        V.tensor_scalar_mul(out=minus_h[:], in0=h[:], scalar1=-1.0)
-        h_sq = const("h_sq")
-        V.tensor_tensor(out=h_sq[:], in0=h[:], in1=h[:], op=AL.mult)
-        y2 = const("y2")
-        V.tensor_tensor(out=y2[:], in0=h_sq[:], in1=sb[:], op=AL.mult)
-        minus_y2 = const("minus_y2")
-        V.tensor_scalar_mul(out=minus_y2[:], in0=y2[:], scalar1=-1.0)
-        one_plus_y2 = const("one_plus_y2")
-        V.tensor_scalar_add(out=one_plus_y2[:], in0=y2[:], scalar1=1.0)
-        clamp_slope = const("clamp_slope")
-        V.tensor_scalar(out=clamp_slope[:], in0=y2[:], scalar1=-1.0 / MAX_NORM2, scalar2=1.0 / MAX_NORM2, op0=AL.mult, op1=AL.add)
+        def rows(name):
+            return keep.tile([P, NT], F32, name=name)
 
-        def transpose_pair(pair):
-            grouped = grouped_pool.tile([P, 2, K], BF16, name="grouped", align_bytes=64)
-            transposed = []
-            for j in range(2):
-                words = x_tiles[2 * pair + j].bitcast(F32)
-                bank = ps_transposed.tile([P, 2 * PASSES, P], F32, name="transposed")
-                transposed.append(bank)
-                for g in range(PASSES):
-                    for u in range(2):
-                        nc.tensor.transpose(bank[:, 2 * g + u, :], words[:, 256 * g + u : 256 * (g + 1) : 2], identity[:])
-            for j in range(2):
-                dst = grouped[:, j, :].bitcast(F32).rearrange("p (g r u) -> p g r u", g=PASSES, u=2)
-                src = transposed[j][:].rearrange("p (g u) r -> p g r u", g=PASSES)
-                if pair < VECTOR_PAIRS:
-                    nc.vector.tensor_copy(out=dst, in_=src)
-                else:
-                    nc.scalar.copy(out=dst, in_=src)
+        def bias_numbers(place):
+            sb, sb_floor, inv_bias_norm, bias_norm = const("sb"), const("sb_floor"), const("inv_bias_norm"), const("bias_norm")
+            e_squared, bias_power, inv_e, bias_tanh = const("e_squared"), const("bias_power"), const("inv_e"), const("bias_tanh")
+            h, h_sq, y2, capped = const("h"), const("h_sq"), const("y2"), const("capped")
+            minus_4h, four_y2, eight_y2, one_plus_y2, clamp_slope = const("minus_4h"), const("four_y2"), const("eight_y2"), const("one_plus_y2"), const("clamp_slope")
+
+            def sum_of_squares():
+                squares = unused.tile([P, N], F32, name="bias_squares")
+                V.scalar_tensor_tensor(out=squares[:], in0=bias_all[:], scalar=1.0, in1=bias_all[:], op0=AL.mult, op1=AL.mult, accum_out=sb[:])
+                V.tensor_scalar_add(out=e_squared[:], in0=zero[:], scalar1=math.exp(2.0))
+
+            def norm():
+                V.tensor_scalar_max(out=sb_floor[:], in0=sb[:], scalar1=MIN_SQ)
+                nc.gpsimd.tensor_tensor(out=bias_norm[:], in0=sb_floor[:], in1=half[:], op=AL.pow)
+
+            def power():
+                V.reciprocal(out=inv_bias_norm[:], in_=bias_norm[:])
+                V.tensor_scalar_min(out=capped[:], in0=bias_norm[:], scalar1=30.0)
+                nc.gpsimd.tensor_tensor(out=bias_power[:], in0=e_squared[:], in1=capped[:], op=AL.pow)
+
+            def tanh():
+                V.tensor_scalar_add(out=bias_power[:], in0=bias_power[:], scalar1=1.0)
+                V.reciprocal(out=inv_e[:], in_=bias_power[:])
+                V.tensor_scalar(out=bias_tanh[:], in0=inv_e[:], scalar1=-2.0, scalar2=1.0, op0=AL.mult, op1=AL.add)
+
+            def factors():
+                V.scalar_tensor_tensor(out=h[:], in0=bias_tanh[:], scalar=MAX_NORM, in1=inv_bias_norm[:], op0=AL.min, op1=AL.mult)
+                V.tensor_tensor(out=h_sq[:], in0=h[:], in1=h[:], op=AL.mult)
+                V.tensor_tensor(out=y2[:], in0=h_sq[:], in1=sb[:], op=AL.mult)
+                V.tensor_scalar_mul(out=minus_4h[:], in0=h[:], scalar1=-4.0)
+
+            def constants():
+                V.tensor_scalar_mul(out=four_y2[:], in0=y2[:], scalar1=4.0)
+                V.tensor_scalar_mul(out=eight_y2[:], in0=y2[:], scalar1=8.0)
+                V.tensor_scalar_add(out=one_plus_y2[:], in0=y2[:], scalar1=1.0)
+                V.tensor_scalar(out=clamp_slope[:], in0=y2[:], scalar1=-4.0 / MAX_NORM2, scalar2=4.0 / MAX_NORM2, op0=AL.mult, op1=AL.add)
+
+            for i, call in enumerate([sum_of_squares, norm, power, tanh, factors, constants]):
+                put(place + 2 * i, call)
+            return minus_4h, four_y2, eight_y2, one_plus_y2, clamp_slope
+
+        xn, u, one_minus_u, inv_one_minus_u = rows("xn"), rows("u"), rows("one_minus_u"), rows("inv_one_minus_u")
+        inv_mn, exponent, e_power, e_plus_1, q = rows("inv_mn"), rows("exponent"), rows("e_power"), rows("e_plus_1"), rows("q")
+        sm_over_xn, minus_beta, minus_res, den_part, two_xy = rows("sm_over_xn"), rows("minus_beta"), rows("minus_res"), rows("den_part"), rows("two_xy")
+        den, inv_den, minus_tau, shrink, alpha, unclamped = rows("den"), rows("inv_den"), rows("minus_tau"), rows("shrink"), rows("alpha"), rows("unclamped")
+
+        def x_scalars(place, g):
+            def inverse():
+                nc.scalar.activation(out=inv_xn[:, g], in_=sx[:, g], func=AF.Abs_reciprocal_sqrt, bias=MIN_SQ)
+
+            def norm():
+                V.tensor_tensor(out=xn[:, g], in0=sx[:, g], in1=inv_xn[:, g], op=AL.mult)
+
+            def clamp():
+                V.tensor_scalar_min(out=u[:, g], in0=xn[:, g], scalar1=1.0 - 1e-5)
+
+            def difference():
+                V.tensor_scalar(out=one_minus_u[:, g], in0=u[:, g], scalar1=-1.0, scalar2=1.0, op0=AL.mult, op1=AL.add)
+
+            def invert():
+                V.reciprocal(out=inv_one_minus_u[:, g], in_=one_minus_u[:, g])
+
+            def quotient():
+                V.scalar_tensor_tensor(out=ratio[:, g], in0=u[:, g], scalar=1.0, in1=inv_one_minus_u[:, g], op0=AL.add, op1=AL.mult)
+
+            put(place, inverse)
+            for i, call in enumerate([norm, clamp, difference, invert, quotient]):
+                put(place + 4 + i, call)
+
+        def row_scalars(place, g, count):
+            def add_parts():
+                V.tensor_tensor(out=sums[:, :, g], in0=parts[:, :, g, 0], in1=parts[:, :, g, 1], op=AL.add)
+                nc.scalar.activation(out=inv_mn[:, g], in_=sums[:, 0, g], func=AF.Abs_reciprocal_sqrt, bias=MIN_SQ)
+
+            def over_xn():
+                V.tensor_tensor(out=sm_over_xn[:, g], in0=sums[:, 0, g], in1=inv_xn[:, g], op=AL.mult)
+
+            def power():
+                V.tensor_tensor(out=exponent[:, g], in0=sm_over_xn[:, g], in1=inv_mn[:, g], op=AL.mult)
+                nc.gpsimd.tensor_tensor(out=e_power[:, g], in0=ratio[:, g], in1=exponent[:, g], op=AL.pow)
+
+            def clamp_power():
+                V.tensor_scalar(out=e_plus_1[:, g], in0=e_power[:, g], scalar1=MAX_E, scalar2=1.0, op0=AL.min, op1=AL.add)
+
+            def invert_power():
+                V.reciprocal(out=q[:, g], in_=e_plus_1[:, g])
+
+            def from_q():
+                V.scalar_tensor_tensor(out=minus_beta[:, g], in0=q[:, g], scalar=1.0, in1=q[:, g], op0=AL.subtract, op1=AL.mult)
+                V.scalar_tensor_tensor(out=minus_res[:, g], in0=q[:, g], scalar=0.5, in1=inv_mn[:, g], op0=AL.subtract, op1=AL.mult)
+
+            def denominator_parts():
+                V.tensor_scalar(out=den_part[:, g], in0=minus_beta[:, g], scalar1=four_y2[:], scalar2=one_plus_y2[:], op0=AL.mult, op1=AL.add)
+                V.scalar_tensor_tensor(out=two_xy[:, g], in0=sums[:, 1, g], scalar=minus_4h[:], in1=minus_res[:, g], op0=AL.mult, op1=AL.mult)
+
+            def denominator():
+                V.tensor_tensor(out=den[:, g], in0=den_part[:, g], in1=two_xy[:, g], op=AL.add)
+
+            def invert_denominator():
+                V.reciprocal(out=inv_den[:, g], in_=den[:, g])
+
+            def tau():
+                V.tensor_tensor(out=minus_tau[:, g], in0=minus_beta[:, g], in1=inv_den[:, g], op=AL.mult)
+                nc.scalar.activation(out=shrink[:, g], in_=minus_tau[:, g], func=AF.Abs_reciprocal_sqrt, scale=clamp_slope[:], bias=1.0 / MAX_NORM2)
+
+            def alpha_over_den():
+                V.tensor_scalar(out=alpha[:, g], in0=minus_tau[:, g], scalar1=eight_y2[:], scalar2=-2.0, op0=AL.mult, op1=AL.add)
+
+            def coefficients():
+                V.tensor_tensor(out=unclamped[:, g], in0=alpha[:, g], in1=minus_res[:, g], op=AL.mult)
+                V.scalar_tensor_tensor(out=coef_bias[:, g], in0=shrink[:, g], scalar=1.0, in1=minus_tau[:, g], op0=AL.min, op1=AL.mult)
+
+            def last():
+                V.scalar_tensor_tensor(out=coef_mx[:, g], in0=shrink[:, g], scalar=1.0, in1=unclamped[:, g], op0=AL.min, op1=AL.mult)
+
+            def for_scalar():
+                V.tensor_scalar(out=full_coef_bias[:, g], in0=coef_bias[:, g], scalar1=minus_4h[:], scalar2=1.0, op0=AL.mult, op1=AL.mult)
+
+            calls = {1: add_parts, 2: over_xn, 3: power, 5: clamp_power, 6: invert_power, 7: from_q, 8: denominator_parts, 9: denominator,
+                     10: invert_denominator, 11: tau, 12: alpha_over_den, 13: coefficients, 14: last}
+            for offset, call in calls.items():
+                put(place + offset * (LAG - count) // CHAIN_STEPS, call)
+            if g.stop > DRAIN:
+                put(place + 13 * (LAG - count) // CHAIN_STEPS, for_scalar)
+
+        def transpose_tile(t):
+            words = x_tiles[t].bitcast(F32)
+            transposed = ps_transposed.tile([P, 2 * PASSES, P], F32, name="transposed")
+            for g in range(PASSES):
+                for u in range(2):
+                    nc.tensor.transpose(transposed[:, 2 * g + u, :], words[:, 256 * g + u : 256 * (g + 1) : 2], identity[:])
+            return transposed
+
+        def copy_tile(t, transposed):
+            grouped = grouped_pool.tile([P, K], BF16, name="grouped", align_bytes=64)
+            dst = grouped[:].bitcast(F32).rearrange("p (g r u) -> p g r u", g=PASSES, u=2)
+            src = transposed[:].rearrange("p (g u) r -> p g r u", g=PASSES)
+            if t < VECTOR_COPIES:
+                V.tensor_copy(out=dst, in_=src)
+            else:
+                nc.scalar.copy(out=dst, in_=src)
             return grouped
 
-        def quantise_pair(pair, grouped):
-            tiles = slice(2 * pair, 2 * pair + 2)
-            nc.vector.quantize_mx(
-                out=x_codes[:, tiles, :].rearrange("p a c -> p (a c)").bitcast(FP8X4),
-                scales=x_scales[:, tiles, :].rearrange("p a c -> p (a c)"),
-                in_=grouped[:].rearrange("p a c -> p (a c)"),
-            )
+        def quantise_tile(t, grouped):
+            V.quantize_mx(out=x_codes[:, t, :].bitcast(FP8X4), scales=x_scales[:, t, :], in_=grouped[:])
 
         def x_norm(t):
             squares = unused.tile([P, K], BF16, name="x_squares")
@@ -167,11 +277,11 @@ def tile_hyplinear_kernel(tc, x, weight_words, weight_scales, bias, out):
         def product(t, pool):
             banks = []
             for half_n in range(2):
-                banks.append(pool.tile([P, BANK], F32, name="mx"))
-            for half_n in range(2):
+                bank = pool.tile([P, BANK], F32, name="mx")
+                banks.append(bank)
                 for g in range(PASSES):
                     nc.tensor.matmul_mx(
-                        out=banks[half_n][:],
+                        out=bank[:],
                         lhsT=x_codes[:, t, P * g : P * (g + 1)].bitcast(FP8X4),
                         lhsT_scale=x_scales[:, t, P * g : P * (g + 1)],
                         rhs=w_codes[:, g, 2 * BANK * half_n : 2 * BANK * (half_n + 1)].bitcast(FP4X4),
@@ -181,120 +291,87 @@ def tile_hyplinear_kernel(tc, x, weight_words, weight_scales, bias, out):
                     )
             return banks
 
-        def statistics_sweep(t):
-            banks = product(t, ps_stats)
+        def sum_of_squares(t, bank, half_n):
+            squares = unused.tile([P, BANK], BF16, name="mx_squares")
+            nc.scalar.activation(out=squares[:], in_=bank[:], func=AF.Square, accum_out=parts[:, 0, t, half_n : half_n + 1])
 
-            def sum_of_squares(half_n):
-                squares = unused.tile([P, BANK], BF16, name="mx_squares")
-                nc.scalar.activation(out=squares[:], in_=banks[half_n][:], func=AF.Square, accum_out=sm[:, t, half_n : half_n + 1])
+        def dot_with_bias(t, bank, half_n):
+            products = unused.tile([P, BANK], F32, name="products")
+            V.scalar_tensor_tensor(
+                out=products[:], in0=bank[:], scalar=1.0, in1=bias_all[:, BANK * half_n : BANK * (half_n + 1)],
+                op0=AL.mult, op1=AL.mult, accum_out=parts[:, 1, t, half_n : half_n + 1],
+            )
 
-            def dot_with_bias(half_n):
-                products = unused.tile([P, BANK], F32, name="products")
-                nc.vector.scalar_tensor_tensor(
-                    out=products[:], in0=banks[half_n][:], scalar=1.0, in1=bias_all[:, BANK * half_n : BANK * (half_n + 1)],
-                    op0=AL.mult, op1=AL.mult, accum_out=d[:, t, half_n : half_n + 1],
-                )
-
-            sum_of_squares(0)
-            dot_with_bias(1)
-            sum_of_squares(1)
-            dot_with_bias(0)
-
-        def tmp(name):
-            return small.tile([P, GROUP], F32, name=name)
-
-        def x_scalars(first):
-            g = slice(first, first + GROUP)
-            xn = tmp("xn")
-            nc.scalar.activation(out=xn[:], in_=sx[:, g], func=AF.Sqrt, bias=MIN_SQ)
-            u = tmp("u")
-            V.tensor_scalar_min(out=u[:], in0=xn[:], scalar1=1.0 - 1e-5)
-            V.reciprocal(out=inv_xn[:, g], in_=xn[:])
-            one_minus_u = tmp("one_minus_u")
-            nc.scalar.activation(out=one_minus_u[:], in_=u[:], func=AF.Identity, scale=-1.0, bias=1.0)
-            inv_one_minus_u = tmp("inv_one_minus_u")
-            V.reciprocal(out=inv_one_minus_u[:], in_=one_minus_u[:])
-            V.scalar_tensor_tensor(out=ratio[:, g], in0=u[:], scalar=1.0, in1=inv_one_minus_u[:], op0=AL.add, op1=AL.mult)
-
-        def row_scalars(first):
-            g = slice(first, first + GROUP)
-            sm_floor = tmp("sm_floor")
-            V.scalar_tensor_tensor(out=sm_floor[:], in0=sm[:, g, 0], scalar=MIN_SQ, in1=sm[:, g, 1], op0=AL.max, op1=AL.add)
-            mn = tmp("mn")
-            nc.scalar.activation(out=mn[:], in_=sm_floor[:], func=AF.Sqrt)
-            d_sum = tmp("d_sum")
-            V.tensor_tensor(out=d_sum[:], in0=d[:, g, 0], in1=d[:, g, 1], op=AL.add)
-            exponent = tmp("exponent")
-            V.tensor_tensor(out=exponent[:], in0=mn[:], in1=inv_xn[:, g], op=AL.mult)
-            e_pow = tmp("e_pow")
-            nc.gpsimd.tensor_tensor(out=e_pow[:], in0=ratio[:, g], in1=exponent[:], op=AL.pow)
-            inv_mn = tmp("inv_mn")
-            V.reciprocal(out=inv_mn[:], in_=mn[:])
-            e_plus_1 = tmp("e_plus_1")
-            V.tensor_scalar(out=e_plus_1[:], in0=e_pow[:], scalar1=1e30, scalar2=1.0, op0=AL.min, op1=AL.add)
-            inv_e = tmp("inv_e")
-            V.reciprocal(out=inv_e[:], in_=e_plus_1[:])
-            rho_minus_1 = tmp("rho_minus_1")
-            V.tensor_scalar(out=rho_minus_1[:], in0=inv_e[:], scalar1=(1.0 - MAX_NORM) / 2.0, scalar2=-2.0, op0=AL.max, op1=AL.mult)
-            minus_beta = tmp("minus_beta")
-            V.scalar_tensor_tensor(out=minus_beta[:], in0=rho_minus_1[:], scalar=2.0, in1=rho_minus_1[:], op0=AL.add, op1=AL.mult)
-            res_scale = tmp("res_scale")
-            V.scalar_tensor_tensor(out=res_scale[:], in0=rho_minus_1[:], scalar=1.0, in1=inv_mn[:], op0=AL.add, op1=AL.mult)
-            den_part = tmp("den_part")
-            nc.scalar.activation(out=den_part[:], in_=minus_beta[:], func=AF.Identity, scale=y2[:], bias=one_plus_y2[:])
-            two_xy = tmp("two_xy")
-            V.scalar_tensor_tensor(out=two_xy[:], in0=d_sum[:], scalar=two_h[:], in1=res_scale[:], op0=AL.mult, op1=AL.mult)
-            den = tmp("den")
-            V.tensor_tensor(out=den[:], in0=den_part[:], in1=two_xy[:], op=AL.add)
-            inv_den = tmp("inv_den")
-            V.reciprocal(out=inv_den[:], in_=den[:])
-            minus_tau = tmp("minus_tau")
-            V.tensor_tensor(out=minus_tau[:], in0=minus_beta[:], in1=inv_den[:], op=AL.mult)
-            excess = tmp("excess")
-            nc.scalar.activation(out=excess[:], in_=minus_tau[:], func=AF.Relu, scale=clamp_slope[:], bias=1.0 / MAX_NORM2 - 1.0)
-            shrink = tmp("shrink")
-            nc.scalar.activation(out=shrink[:], in_=excess[:], func=AF.Sqrt, bias=1.0)
-            alpha_over_den = tmp("alpha_over_den")
-            nc.scalar.activation(out=alpha_over_den[:], in_=minus_tau[:], func=AF.Identity, scale=minus_y2[:], bias=1.0)
-            unclamped_a = tmp("unclamped_a")
-            V.tensor_tensor(out=unclamped_a[:], in0=alpha_over_den[:], in1=res_scale[:], op=AL.mult)
-            inv_shrink = tmp("inv_shrink")
-            V.reciprocal(out=inv_shrink[:], in_=shrink[:])
-            V.tensor_tensor(out=coef_mx[:, g], in0=unclamped_a[:], in1=inv_shrink[:], op=AL.mult)
-            V.scalar_tensor_tensor(out=coef_bias[:, g], in0=minus_tau[:], scalar=minus_h[:], in1=inv_shrink[:], op0=AL.mult, op1=AL.mult)
-
-        def output_sweep(t):
-            bias_term = bias_term_pool.tile([P, N], F32, name="bias_term")
-            nc.gpsimd.tensor_scalar(out=bias_term[:], in0=bias_all[:], scalar1=coef_bias[:, t : t + 1], scalar2=0.0, op0=AL.mult, op1=AL.add)
-            banks = product(t, ps_out)
-            out_tile = out_pool.tile([P, N], F32, name="out_tile")
+        def spread_bias():
             for half_n in range(2):
                 cols = slice(BANK * half_n, BANK * (half_n + 1))
-                nc.vector.scalar_tensor_tensor(
-                    out=out_tile[:, cols], in0=banks[half_n][:], scalar=coef_mx[:, t : t + 1], in1=bias_term[:, cols], op0=AL.mult, op1=AL.add
-                )
-            nc.sync.dma_start(out=out_rows[:, t, :], in_=out_tile[:])
+                spread = ps_out.tile([P, BANK], F32, name="mx")
+                nc.tensor.matmul(out=spread[:], lhsT=ones[:], rhs=bias_row[:, cols], start=True, stop=True)
+                V.tensor_copy(out=bias_all[:, cols], in_=spread[:])
 
-        with_scalars = 0
-        finished = 0
-        step = 0
-        grouped = None
-        while finished < NT:
-            stats_tile = step - LEAD
-            if step % 2 == 0 and step < NT:
-                grouped = transpose_pair(step // 2)
-            if step < NT:
-                x_norm(step)
-                if step % GROUP == GROUP - 1:
-                    x_scalars(step - GROUP + 1)
-            if 0 <= stats_tile < NT:
-                statistics_sweep(stats_tile)
-            if finished < with_scalars:
-                output_sweep(finished)
-                finished += 1
-            if step % 2 == 0 and step < NT:
-                quantise_pair(step // 2, grouped)
-            if 0 <= stats_tile < NT and stats_tile % GROUP == GROUP - 1:
-                row_scalars(stats_tile - GROUP + 1)
-                with_scalars = stats_tile + 1
-            step += 1
+        def make_bias_term(t):
+            bias_term = bias_term_pool.tile([P, N], F32, name="bias_term")
+            if t > DRAIN and t % 2 == 1:
+                nc.scalar.activation(out=bias_term[:], in_=bias_all[:], func=AF.Copy, scale=full_coef_bias[:, t : t + 1])
+            else:
+                nc.gpsimd.tensor_scalar(out=bias_term[:], in0=bias_all[:], scalar1=coef_bias[:, t : t + 1], scalar2=minus_4h[:], op0=AL.mult, op1=AL.mult)
+            return bias_term
+
+        def write_half(t, bank, bias_term, out_tile, half_n):
+            cols = slice(BANK * half_n, BANK * (half_n + 1))
+            V.scalar_tensor_tensor(
+                out=out_tile[:, cols], in0=bank[:], scalar=coef_mx[:, t : t + 1], in1=bias_term[:, cols], op0=AL.mult, op1=AL.add
+            )
+
+        minus_4h, four_y2, eight_y2, one_plus_y2, clamp_slope = bias_numbers(2)
+        first = 0
+        for count in GROUPS:
+            last_tile = first + count - 1
+            x_scalars(SLOTS * (last_tile + 1 - SQUARES_LEAD) + 1, slice(first, first + count))
+            row_scalars(SLOTS * (last_tile + 1), slice(first, first + count), count)
+            first += count
+
+        grouped = {}
+        stats_banks = {}
+        out_banks = {}
+        bias_terms = {}
+        for step in range(-SQUARES_LEAD, NT + LAG):
+            multiplied = step + 1
+            quantised = step + 2
+            turned = step + 3
+            written = step - LAG
+            place = SLOTS * step
+            if 0 <= turned < NT:
+                transposed = transpose_tile(turned)
+            if 0 <= multiplied < NT:
+                stats_banks[multiplied] = product(multiplied, ps_stats)
+            run_place(place)
+            if 0 <= quantised < NT:
+                quantise_tile(quantised, grouped[quantised])
+            run_place(place + 1)
+            if step == 0:
+                spread_bias()
+            if 0 <= turned < VECTOR_COPIES:
+                grouped[turned] = copy_tile(turned, transposed)
+            if written >= 0:
+                out_tile = out_pool.tile([P, N], F32, name="out_tile")
+                write_half(written, out_banks[written][0], bias_terms[written], out_tile, 0)
+            run_place(place + 2)
+            if written >= 0:
+                write_half(written, out_banks[written][1], bias_terms[written], out_tile, 1)
+                nc.sync.dma_start(out=out_rows[:, written, :], in_=out_tile[:])
+            run_place(place + 3)
+            if 0 <= written + 1 < NT:
+                bias_terms[written + 1] = make_bias_term(written + 1)
+                out_banks[written + 1] = product(written + 1, ps_out)
+            if 0 <= step < NT:
+                sum_of_squares(step, stats_banks[step][0], 0)
+                sum_of_squares(step, stats_banks[step][1], 1)
+                dot_with_bias(step, stats_banks[step][0], 0)
+            run_place(place + 4)
+            if 0 <= step < NT:
+                dot_with_bias(step, stats_banks[step][1], 1)
+            if VECTOR_COPIES <= turned < NT:
+                grouped[turned] = copy_tile(turned, transposed)
+            if step + SQUARES_LEAD < NT:
+                x_norm(step + SQUARES_LEAD)

@@ -29,7 +29,7 @@ MIN_SQ = 1e-15
 MAX_E = 2.0 / (1.0 - MAX_NORM) - 1.0
 
 X_LOADS = [1, 1, 2, 4, 4, 4, 4, 4, 4, 4]
-GROUPS = [4, 4, 4, 4, 4, 4, 4, 2, 2]
+GROUPS = [8, 8, 8, 8]
 SLOTS = 5
 CHAIN_STEPS = 3
 LAG = max(GROUPS) + CHAIN_STEPS

@@ -28,13 +28,13 @@ MAX_NORM2 = MAX_NORM * MAX_NORM
 MIN_SQ = 1e-15
 MAX_E = 2.0 / (1.0 - MAX_NORM) - 1.0
 
-X_LOADS = [1, 1, 2, 4, 4, 4, 4, 4, 4, 4]
+X_LOADS = [1, 1, 1, 1, 2, 2, 4, 4, 4, 4, 4, 4]
 GROUPS = [8, 8, 8, 8]
 SLOTS = 5
 CHAIN_STEPS = 3
 LAG = max(GROUPS) + CHAIN_STEPS
 DRAIN = NT - LAG
-SQUARES_LEAD = 4
+SQUARES_LEAD = 3
 VECTOR_COPIES = 8
 
 
@@ -84,16 +84,16 @@ def tile_hyplinear_kernel(tc, x, weight_words, weight_scales, bias, out):
             nc.sync.dma_start(out=loaded[:], in_=x_rows[:, first : first + count, :])
 
         load_x(0)
+        nc.sync.dma_start(out=bias_row[0:1, :], in_=bias.rearrange("(o n) -> o n", o=1))
+        load_x(1)
         scales32 = weight_scales.bitcast(I32)
         for quadrant in range(4):
             nc.sync.dma_start(
                 out=w_scales[32 * quadrant : 32 * quadrant + 4].bitcast(I32),
                 in_=scales32[:, 4 * quadrant : 4 * quadrant + 4, :].rearrange("g r n -> r g n"),
             )
-        load_x(1)
         w_codes = keep.tile([P, PASSES, 2 * N], U8, align_bytes=64)
         nc.sync.dma_start(out=w_codes[:].bitcast(I32), in_=weight_words.bitcast(I32).rearrange("g p n -> p g n"))
-        nc.sync.dma_start(out=bias_row[0:1, :], in_=bias.rearrange("(o n) -> o n", o=1))
         for i in range(2, len(X_LOADS)):
             load_x(i)
 
@@ -105,7 +105,6 @@ def tile_hyplinear_kernel(tc, x, weight_words, weight_scales, bias, out):
         sums = keep.tile([P, 2, NT], F32)
         coef_mx = keep.tile([P, NT], F32)
         coef_bias = keep.tile([P, NT], F32)
-        full_coef_bias = keep.tile([P, NT], F32)
         inv_xn = keep.tile([P, NT], F32)
         ratio = keep.tile([P, NT], F32)
 
@@ -169,6 +168,7 @@ def tile_hyplinear_kernel(tc, x, weight_words, weight_scales, bias, out):
         inv_mn, exponent, e_power, e_plus_1, q = rows("inv_mn"), rows("exponent"), rows("e_power"), rows("e_plus_1"), rows("q")
         sm_over_xn, minus_beta, minus_res, den_part, two_xy = rows("sm_over_xn"), rows("minus_beta"), rows("minus_res"), rows("den_part"), rows("two_xy")
         den, inv_den, minus_tau, shrink, alpha, unclamped = rows("den"), rows("inv_den"), rows("minus_tau"), rows("shrink"), rows("alpha"), rows("unclamped")
+        h_tau = rows("h_tau")
 
         def x_scalars(place, g):
             def inverse():
@@ -229,25 +229,20 @@ def tile_hyplinear_kernel(tc, x, weight_words, weight_scales, bias, out):
                 V.tensor_tensor(out=minus_tau[:, g], in0=minus_beta[:, g], in1=inv_den[:, g], op=AL.mult)
                 nc.scalar.activation(out=shrink[:, g], in_=minus_tau[:, g], func=AF.Abs_reciprocal_sqrt, scale=clamp_slope[:], bias=1.0 / MAX_NORM2)
 
-            def alpha_over_den():
-                V.tensor_scalar(out=alpha[:, g], in0=minus_tau[:, g], scalar1=eight_y2[:], scalar2=-2.0, op0=AL.mult, op1=AL.add)
-
             def coefficients():
-                V.tensor_tensor(out=unclamped[:, g], in0=alpha[:, g], in1=minus_res[:, g], op=AL.mult)
-                V.scalar_tensor_tensor(out=coef_bias[:, g], in0=shrink[:, g], scalar=1.0, in1=minus_tau[:, g], op0=AL.min, op1=AL.mult)
+                V.tensor_scalar(out=alpha[:, g], in0=minus_tau[:, g], scalar1=eight_y2[:], scalar2=-2.0, op0=AL.mult, op1=AL.add)
+                V.tensor_scalar(out=h_tau[:, g], in0=minus_tau[:, g], scalar1=minus_4h[:], scalar2=1.0, op0=AL.mult, op1=AL.mult)
 
             def last():
+                V.tensor_tensor(out=unclamped[:, g], in0=alpha[:, g], in1=minus_res[:, g], op=AL.mult)
+                V.scalar_tensor_tensor(out=coef_bias[:, g], in0=shrink[:, g], scalar=1.0, in1=h_tau[:, g], op0=AL.min, op1=AL.mult)
                 V.scalar_tensor_tensor(out=coef_mx[:, g], in0=shrink[:, g], scalar=1.0, in1=unclamped[:, g], op0=AL.min, op1=AL.mult)
 
-            def for_scalar():
-                V.tensor_scalar(out=full_coef_bias[:, g], in0=coef_bias[:, g], scalar1=minus_4h[:], scalar2=1.0, op0=AL.mult, op1=AL.mult)
 
             calls = {1: add_parts, 2: over_xn, 3: power, 5: clamp_power, 6: invert_power, 7: from_q, 8: denominator_parts, 9: denominator,
-                     10: invert_denominator, 11: tau, 12: alpha_over_den, 13: coefficients, 14: last}
+                     10: invert_denominator, 11: tau, 12: coefficients, 13: last}
             for offset, call in calls.items():
                 put(place + offset * (LAG - count) // CHAIN_STEPS, call)
-            if g.stop > DRAIN:
-                put(place + 13 * (LAG - count) // CHAIN_STEPS, for_scalar)
 
         def transpose_tile(t):
             words = x_tiles[t].bitcast(F32)
@@ -312,9 +307,9 @@ def tile_hyplinear_kernel(tc, x, weight_words, weight_scales, bias, out):
         def make_bias_term(t):
             bias_term = bias_term_pool.tile([P, N], F32, name="bias_term")
             if t > DRAIN and t % 2 == 1:
-                nc.scalar.activation(out=bias_term[:], in_=bias_all[:], func=AF.Copy, scale=full_coef_bias[:, t : t + 1])
+                nc.scalar.activation(out=bias_term[:], in_=bias_all[:], func=AF.Copy, scale=coef_bias[:, t : t + 1])
             else:
-                nc.gpsimd.tensor_scalar(out=bias_term[:], in0=bias_all[:], scalar1=coef_bias[:, t : t + 1], scalar2=minus_4h[:], op0=AL.mult, op1=AL.mult)
+                nc.gpsimd.tensor_scalar(out=bias_term[:], in0=bias_all[:], scalar1=coef_bias[:, t : t + 1], scalar2=0.0, op0=AL.mult, op1=AL.add)
             return bias_term
 
         def write_half(t, bank, bias_term, out_tile, half_n):
@@ -323,7 +318,7 @@ def tile_hyplinear_kernel(tc, x, weight_words, weight_scales, bias, out):
                 out=out_tile[:, cols], in0=bank[:], scalar=coef_mx[:, t : t + 1], in1=bias_term[:, cols], op0=AL.mult, op1=AL.add
             )
 
-        minus_4h, four_y2, eight_y2, one_plus_y2, clamp_slope = bias_numbers(2)
+        minus_4h, four_y2, eight_y2, one_plus_y2, clamp_slope = bias_numbers(0)
         first = 0
         for count in GROUPS:
             last_tile = first + count - 1
@@ -335,21 +330,23 @@ def tile_hyplinear_kernel(tc, x, weight_words, weight_scales, bias, out):
         stats_banks = {}
         out_banks = {}
         bias_terms = {}
-        for step in range(-SQUARES_LEAD, NT + LAG):
+        for step in range(-3, NT + LAG):
             multiplied = step + 1
             quantised = step + 2
             turned = step + 3
             written = step - LAG
             place = SLOTS * step
+            if step == -1:
+                stats_banks[multiplied] = product(multiplied, ps_stats)
             if 0 <= turned < NT:
                 transposed = transpose_tile(turned)
-            if 0 <= multiplied < NT:
+            if 1 <= multiplied < NT:
                 stats_banks[multiplied] = product(multiplied, ps_stats)
             run_place(place)
             if 0 <= quantised < NT:
                 quantise_tile(quantised, grouped[quantised])
             run_place(place + 1)
-            if step == 0:
+            if step == -1:
                 spread_bias()
             if 0 <= turned < VECTOR_COPIES:
                 grouped[turned] = copy_tile(turned, transposed)
@@ -373,5 +370,5 @@ def tile_hyplinear_kernel(tc, x, weight_words, weight_scales, bias, out):
                 dot_with_bias(step, stats_banks[step][1], 1)
             if VECTOR_COPIES <= turned < NT:
                 grouped[turned] = copy_tile(turned, transposed)
-            if step + SQUARES_LEAD < NT:
+            if 0 <= step + SQUARES_LEAD < NT:
                 x_norm(step + SQUARES_LEAD)

@@ -29,7 +29,7 @@ MIN_SQ = 1e-15
 MAX_E = 2.0 / (1.0 - MAX_NORM) - 1.0
 
 X_LOADS = [1, 1, 1, 1, 2, 2, 4, 4, 4, 4, 4, 4]
-GROUPS = [8, 8, 8, 8]
+GROUPS = [8, 8, 8, 4, 4]
 SLOTS = 5
 CHAIN_STEPS = 3
 LAG = max(GROUPS) + CHAIN_STEPS
@@ -46,8 +46,8 @@ def tile_hyplinear_kernel(tc, x, weight_words, weight_scales, bias, out):
     with ExitStack() as ctx:
         keep = ctx.enter_context(tc.tile_pool(name="keep", bufs=1))
         grouped_pool = ctx.enter_context(tc.tile_pool(name="grouped", bufs=3))
-        unused = ctx.enter_context(tc.tile_pool(name="unused", bufs=2))
-        bias_term_pool = ctx.enter_context(tc.tile_pool(name="bias_term", bufs=2))
+        unused = ctx.enter_context(tc.tile_pool(name="unused", bufs=6))
+        bias_term_pool = ctx.enter_context(tc.tile_pool(name="bias_term", bufs=3))
         out_pool = ctx.enter_context(tc.tile_pool(name="out_tile", bufs=4))
         ps_transposed = ctx.enter_context(tc.psum_pool(name="ps_transposed", bufs=1))
         ps_stats = ctx.enter_context(tc.psum_pool(name="ps_stats", bufs=4))
@@ -60,12 +60,12 @@ def tile_hyplinear_kernel(tc, x, weight_words, weight_scales, bias, out):
         nc.scalar.activation(out=warm[:], in_=warm[:], func=AF.Abs_reciprocal_sqrt)
         identity = keep.tile([P, P], F32)
         make_identity(nc, identity[:])
-        w_scales = keep.tile([P, PASSES, N], U8, align_bytes=64)
-        V.memset(w_scales[:].bitcast(I32), 0)
         bias_row = keep.tile([P, N], BF16)
         V.memset(bias_row[:], 0.0)
         ones = keep.tile([P, P], BF16)
         V.memset(ones[:], 1.0)
+        w_scales = keep.tile([P, PASSES, N], U8, align_bytes=64)
+        V.memset(w_scales[:].bitcast(I32), 0)
         zero = keep.tile([P, 1], F32)
         V.memset(zero[:], 0.0)
         half = keep.tile([P, 1], F32)
@@ -84,8 +84,8 @@ def tile_hyplinear_kernel(tc, x, weight_words, weight_scales, bias, out):
             nc.sync.dma_start(out=loaded[:], in_=x_rows[:, first : first + count, :])
 
         load_x(0)
-        nc.sync.dma_start(out=bias_row[0:1, :], in_=bias.rearrange("(o n) -> o n", o=1))
         load_x(1)
+        nc.sync.dma_start(out=bias_row[0:1, :], in_=bias.rearrange("(o n) -> o n", o=1))
         scales32 = weight_scales.bitcast(I32)
         for quadrant in range(4):
             nc.sync.dma_start(
@@ -130,7 +130,7 @@ def tile_hyplinear_kernel(tc, x, weight_words, weight_scales, bias, out):
             minus_4h, four_y2, eight_y2, one_plus_y2, clamp_slope = const("minus_4h"), const("four_y2"), const("eight_y2"), const("one_plus_y2"), const("clamp_slope")
 
             def sum_of_squares():
-                squares = unused.tile([P, N], F32, name="bias_squares")
+                squares = keep.tile([P, N], F32, name="bias_squares")
                 V.scalar_tensor_tensor(out=squares[:], in0=bias_all[:], scalar=1.0, in1=bias_all[:], op0=AL.mult, op1=AL.mult, accum_out=sb[:])
                 V.tensor_scalar_add(out=e_squared[:], in0=zero[:], scalar1=math.exp(2.0))
 
@@ -229,20 +229,19 @@ def tile_hyplinear_kernel(tc, x, weight_words, weight_scales, bias, out):
                 V.tensor_tensor(out=minus_tau[:, g], in0=minus_beta[:, g], in1=inv_den[:, g], op=AL.mult)
                 nc.scalar.activation(out=shrink[:, g], in_=minus_tau[:, g], func=AF.Abs_reciprocal_sqrt, scale=clamp_slope[:], bias=1.0 / MAX_NORM2)
 
-            def coefficients():
+            def last():
                 V.tensor_scalar(out=alpha[:, g], in0=minus_tau[:, g], scalar1=eight_y2[:], scalar2=-2.0, op0=AL.mult, op1=AL.add)
                 V.tensor_scalar(out=h_tau[:, g], in0=minus_tau[:, g], scalar1=minus_4h[:], scalar2=1.0, op0=AL.mult, op1=AL.mult)
 
-            def last():
                 V.tensor_tensor(out=unclamped[:, g], in0=alpha[:, g], in1=minus_res[:, g], op=AL.mult)
                 V.scalar_tensor_tensor(out=coef_bias[:, g], in0=shrink[:, g], scalar=1.0, in1=h_tau[:, g], op0=AL.min, op1=AL.mult)
                 V.scalar_tensor_tensor(out=coef_mx[:, g], in0=shrink[:, g], scalar=1.0, in1=unclamped[:, g], op0=AL.min, op1=AL.mult)
 
+            calls = {1: add_parts, 2: over_xn, 3: power, 6: clamp_power, 7: invert_power, 8: from_q, 9: denominator_parts, 10: denominator,
+                     11: invert_denominator, 12: tau, 13: last}
 
-            calls = {1: add_parts, 2: over_xn, 3: power, 5: clamp_power, 6: invert_power, 7: from_q, 8: denominator_parts, 9: denominator,
-                     10: invert_denominator, 11: tau, 12: coefficients, 13: last}
             for offset, call in calls.items():
-                put(place + offset * (LAG - count) // CHAIN_STEPS, call)
+                put(place + offset * min(LAG - count, CHAIN_STEPS + 3) // CHAIN_STEPS, call)
 
         def transpose_tile(t):
             words = x_tiles[t].bitcast(F32)
@@ -346,7 +345,7 @@ def tile_hyplinear_kernel(tc, x, weight_words, weight_scales, bias, out):
             if 0 <= quantised < NT:
                 quantise_tile(quantised, grouped[quantised])
             run_place(place + 1)
-            if step == -1:
+            if step == -2:
                 spread_bias()
             if 0 <= turned < VECTOR_COPIES:
                 grouped[turned] = copy_tile(turned, transposed)

@@ -30,7 +30,7 @@ MAX_E = 2.0 / (1.0 - MAX_NORM) - 1.0
 
 X_LOADS = [1, 1, 1, 1, 2, 2, 4, 4, 4, 4, 4, 4]
 GROUPS = [8, 8, 8, 4, 4]
-SLOTS = 5
+SLOTS = 4
 CHAIN_STEPS = 3
 LAG = max(GROUPS) + CHAIN_STEPS
 DRAIN = NT - LAG
@@ -108,6 +108,7 @@ def tile_hyplinear_kernel(tc, x, weight_words, weight_scales, bias, out):
         inv_xn = keep.tile([P, NT], F32)
         ratio = keep.tile([P, NT], F32)
 
+        known = {}
         waiting = {}
 
         def put(place, call):
@@ -116,6 +117,13 @@ def tile_hyplinear_kernel(tc, x, weight_words, weight_scales, bias, out):
         def run_place(place):
             for call in waiting.get(place, []):
                 call()
+
+        for_scalar = []
+
+        def run_for_scalar():
+            for call in for_scalar:
+                call()
+            for_scalar.clear()
 
         def const(name):
             return keep.tile([P, 1], F32, name=name)
@@ -172,7 +180,7 @@ def tile_hyplinear_kernel(tc, x, weight_words, weight_scales, bias, out):
 
         def x_scalars(place, g):
             def inverse():
-                nc.scalar.activation(out=inv_xn[:, g], in_=sx[:, g], func=AF.Abs_reciprocal_sqrt, bias=MIN_SQ)
+                for_scalar.append(lambda: nc.scalar.activation(out=inv_xn[:, g], in_=sx[:, g], func=AF.Abs_reciprocal_sqrt, bias=MIN_SQ))
 
             def norm():
                 V.tensor_tensor(out=xn[:, g], in0=sx[:, g], in1=inv_xn[:, g], op=AL.mult)
@@ -191,12 +199,12 @@ def tile_hyplinear_kernel(tc, x, weight_words, weight_scales, bias, out):
 
             put(place, inverse)
             for i, call in enumerate([norm, clamp, difference, invert, quotient]):
-                put(place + 4 + i, call)
+                put(place + 3 + i, call)
 
         def row_scalars(place, g, count):
             def add_parts():
                 V.tensor_tensor(out=sums[:, :, g], in0=parts[:, :, g, 0], in1=parts[:, :, g, 1], op=AL.add)
-                nc.scalar.activation(out=inv_mn[:, g], in_=sums[:, 0, g], func=AF.Abs_reciprocal_sqrt, bias=MIN_SQ)
+                for_scalar.append(lambda: nc.scalar.activation(out=inv_mn[:, g], in_=sums[:, 0, g], func=AF.Abs_reciprocal_sqrt, bias=MIN_SQ))
 
             def over_xn():
                 V.tensor_tensor(out=sm_over_xn[:, g], in0=sums[:, 0, g], in1=inv_xn[:, g], op=AL.mult)
@@ -214,8 +222,6 @@ def tile_hyplinear_kernel(tc, x, weight_words, weight_scales, bias, out):
             def from_q():
                 V.scalar_tensor_tensor(out=minus_beta[:, g], in0=q[:, g], scalar=1.0, in1=q[:, g], op0=AL.subtract, op1=AL.mult)
                 V.scalar_tensor_tensor(out=minus_res[:, g], in0=q[:, g], scalar=0.5, in1=inv_mn[:, g], op0=AL.subtract, op1=AL.mult)
-
-            def denominator_parts():
                 V.tensor_scalar(out=den_part[:, g], in0=minus_beta[:, g], scalar1=four_y2[:], scalar2=one_plus_y2[:], op0=AL.mult, op1=AL.add)
                 V.scalar_tensor_tensor(out=two_xy[:, g], in0=sums[:, 1, g], scalar=minus_4h[:], in1=minus_res[:, g], op0=AL.mult, op1=AL.mult)
 
@@ -227,7 +233,7 @@ def tile_hyplinear_kernel(tc, x, weight_words, weight_scales, bias, out):
 
             def tau():
                 V.tensor_tensor(out=minus_tau[:, g], in0=minus_beta[:, g], in1=inv_den[:, g], op=AL.mult)
-                nc.scalar.activation(out=shrink[:, g], in_=minus_tau[:, g], func=AF.Abs_reciprocal_sqrt, scale=clamp_slope[:], bias=1.0 / MAX_NORM2)
+                for_scalar.append(lambda: nc.scalar.activation(out=shrink[:, g], in_=minus_tau[:, g], func=AF.Abs_reciprocal_sqrt, scale=clamp_slope[:], bias=1.0 / MAX_NORM2))
 
             def last():
                 V.tensor_scalar(out=alpha[:, g], in0=minus_tau[:, g], scalar1=eight_y2[:], scalar2=-2.0, op0=AL.mult, op1=AL.add)
@@ -237,11 +243,15 @@ def tile_hyplinear_kernel(tc, x, weight_words, weight_scales, bias, out):
                 V.scalar_tensor_tensor(out=coef_bias[:, g], in0=shrink[:, g], scalar=1.0, in1=h_tau[:, g], op0=AL.min, op1=AL.mult)
                 V.scalar_tensor_tensor(out=coef_mx[:, g], in0=shrink[:, g], scalar=1.0, in1=unclamped[:, g], op0=AL.min, op1=AL.mult)
 
-            calls = {1: add_parts, 2: over_xn, 3: power, 6: clamp_power, 7: invert_power, 8: from_q, 9: denominator_parts, 10: denominator,
-                     11: invert_denominator, 12: tau, 13: last}
+            calls = {1: add_parts, 2: over_xn, 3: power, 5: clamp_power, 6: invert_power, 7: from_q, 8: denominator, 9: invert_denominator, 10: tau, 11: last}
 
             for offset, call in calls.items():
-                put(place + offset * min(LAG - count, CHAIN_STEPS + 3) // CHAIN_STEPS, call)
+                at = place + offset * min(LAG - count, CHAIN_STEPS + 3) // CHAIN_STEPS
+                if call == last:
+                    at = (at // SLOTS + 1) * SLOTS - 1
+                put(at, call)
+            for t in range(g.start, g.stop):
+                known[t] = at
 
         def transpose_tile(t):
             words = x_tiles[t].bitcast(F32)
@@ -305,7 +315,7 @@ def tile_hyplinear_kernel(tc, x, weight_words, weight_scales, bias, out):
 
         def make_bias_term(t):
             bias_term = bias_term_pool.tile([P, N], F32, name="bias_term")
-            if t > DRAIN and t % 2 == 1:
+            if t > DRAIN and t % 2 == 0:
                 nc.scalar.activation(out=bias_term[:], in_=bias_all[:], func=AF.Copy, scale=coef_bias[:, t : t + 1])
             else:
                 nc.gpsimd.tensor_scalar(out=bias_term[:], in0=bias_all[:], scalar1=coef_bias[:, t : t + 1], scalar2=0.0, op0=AL.mult, op1=AL.add)
@@ -342,9 +352,6 @@ def tile_hyplinear_kernel(tc, x, weight_words, weight_scales, bias, out):
             if 1 <= multiplied < NT:
                 stats_banks[multiplied] = product(multiplied, ps_stats)
             run_place(place)
-            if 0 <= quantised < NT:
-                quantise_tile(quantised, grouped[quantised])
-            run_place(place + 1)
             if step == -2:
                 spread_bias()
             if 0 <= turned < VECTOR_COPIES:
@@ -352,20 +359,26 @@ def tile_hyplinear_kernel(tc, x, weight_words, weight_scales, bias, out):
             if written >= 0:
                 out_tile = out_pool.tile([P, N], F32, name="out_tile")
                 write_half(written, out_banks[written][0], bias_terms[written], out_tile, 0)
+            run_place(place + 1)
+            if 0 <= quantised < NT:
+                quantise_tile(quantised, grouped[quantised])
             run_place(place + 2)
             if written >= 0:
                 write_half(written, out_banks[written][1], bias_terms[written], out_tile, 1)
                 nc.sync.dma_start(out=out_rows[:, written, :], in_=out_tile[:])
-            run_place(place + 3)
-            if 0 <= written + 1 < NT:
-                bias_terms[written + 1] = make_bias_term(written + 1)
-                out_banks[written + 1] = product(written + 1, ps_out)
             if 0 <= step < NT:
                 sum_of_squares(step, stats_banks[step][0], 0)
-                sum_of_squares(step, stats_banks[step][1], 1)
-                dot_with_bias(step, stats_banks[step][0], 0)
-            run_place(place + 4)
+            run_for_scalar()
             if 0 <= step < NT:
+                sum_of_squares(step, stats_banks[step][1], 1)
+            run_place(place + 3)
+            for t in range(max(written + 1, 0), min(written + 3, NT)):
+                if t not in bias_terms and known[t] <= place + 3:
+                    bias_terms[t] = make_bias_term(t)
+            if 0 <= written + 1 < NT:
+                out_banks[written + 1] = product(written + 1, ps_out)
+            if 0 <= step < NT:
+                dot_with_bias(step, stats_banks[step][0], 0)
                 dot_with_bias(step, stats_banks[step][1], 1)
             if VECTOR_COPIES <= turned < NT:
                 grouped[turned] = copy_tile(turned, transposed)

@@ -307,11 +307,12 @@ def tile_hyplinear_kernel(tc, x, weight_words, weight_scales, bias, out):
             )
 
         def spread_bias():
+            spread = []
             for half_n in range(2):
-                cols = slice(BANK * half_n, BANK * (half_n + 1))
-                spread = ps_out.tile([P, BANK], F32, name="mx")
-                nc.tensor.matmul(out=spread[:], lhsT=ones[:], rhs=bias_row[:, cols], start=True, stop=True)
-                V.tensor_copy(out=bias_all[:, cols], in_=spread[:])
+                bank = ps_out.tile([P, BANK], F32, name="mx")
+                nc.tensor.matmul(out=bank[:], lhsT=ones[:], rhs=bias_row[:, BANK * half_n : BANK * (half_n + 1)], start=True, stop=True)
+                spread.append(bank)
+            return spread
 
         def make_bias_term(t):
             bias_term = bias_term_pool.tile([P, N], F32, name="bias_term")
@@ -327,7 +328,7 @@ def tile_hyplinear_kernel(tc, x, weight_words, weight_scales, bias, out):
                 out=out_tile[:, cols], in0=bank[:], scalar=coef_mx[:, t : t + 1], in1=bias_term[:, cols], op0=AL.mult, op1=AL.add
             )
 
-        minus_4h, four_y2, eight_y2, one_plus_y2, clamp_slope = bias_numbers(0)
+        minus_4h, four_y2, eight_y2, one_plus_y2, clamp_slope = bias_numbers(4 * SLOTS)
         first = 0
         for count in GROUPS:
             last_tile = first + count - 1
@@ -349,13 +350,11 @@ def tile_hyplinear_kernel(tc, x, weight_words, weight_scales, bias, out):
                 stats_banks[multiplied] = product(multiplied, ps_stats)
             if 0 <= turned < NT:
                 transposed = transpose_tile(turned)
+            if step == -3:
+                spread = spread_bias()
             if 1 <= multiplied < NT:
                 stats_banks[multiplied] = product(multiplied, ps_stats)
             run_place(place)
-            if step == -2:
-                spread_bias()
-            if 0 <= turned < VECTOR_COPIES:
-                grouped[turned] = copy_tile(turned, transposed)
             if written >= 0:
                 out_tile = out_pool.tile([P, N], F32, name="out_tile")
                 write_half(written, out_banks[written][0], bias_terms[written], out_tile, 0)
@@ -363,6 +362,11 @@ def tile_hyplinear_kernel(tc, x, weight_words, weight_scales, bias, out):
             if 0 <= quantised < NT:
                 quantise_tile(quantised, grouped[quantised])
             run_place(place + 2)
+            if step == -2:
+                for half_n in range(2):
+                    V.tensor_copy(out=bias_all[:, BANK * half_n : BANK * (half_n + 1)], in_=spread[half_n][:])
+            if 0 <= turned < VECTOR_COPIES:
+                grouped[turned] = copy_tile(turned, transposed)
             if written >= 0:
                 write_half(written, out_banks[written][1], bias_terms[written], out_tile, 1)
                 nc.sync.dma_start(out=out_rows[:, written, :], in_=out_tile[:])

@@ -34,8 +34,9 @@ SLOTS = 4
 CHAIN_STEPS = 3
 LAG = max(GROUPS) + CHAIN_STEPS
 DRAIN = NT - LAG
+GRAM = range(4, 14, 2)
 SQUARES_LEAD = 3
-VECTOR_COPIES = 8
+VECTOR_COPIES = 6
 
 
 def tile_hyplinear_kernel(tc, x, weight_words, weight_scales, bias, out):
@@ -274,6 +275,18 @@ def tile_hyplinear_kernel(tc, x, weight_words, weight_scales, bias, out):
         def quantise_tile(t, grouped):
             V.quantize_mx(out=x_codes[:, t, :].bitcast(FP8X4), scales=x_scales[:, t, :], in_=grouped[:])
 
+        def gram(t):
+            columns = grouped[t][:].rearrange("p (g r e) -> p g e r", g=PASSES, e=4)
+            bank = ps_out.tile([P, P], F32, name="mx")
+            for g in range(PASSES):
+                for e in range(4):
+                    nc.tensor.matmul(out=bank[:], lhsT=columns[:, g, e, :], rhs=columns[:, g, e, :], start=(g + e == 0), stop=(g == PASSES - 1 and e == 3))
+            return bank
+
+        def diagonal(t, bank):
+            picked = unused.tile([P, P], F32, name="picked")
+            V.scalar_tensor_tensor(out=picked[:], in0=bank[:], scalar=1.0, in1=identity[:], op0=AL.mult, op1=AL.mult, accum_out=sx[:, t : t + 1])
+
         def x_norm(t):
             squares = unused.tile([P, K], BF16, name="x_squares")
             nc.scalar.activation(out=squares[:], in_=x_tiles[t], func=AF.Square, accum_out=sx[:, t : t + 1])
@@ -340,6 +353,7 @@ def tile_hyplinear_kernel(tc, x, weight_words, weight_scales, bias, out):
         stats_banks = {}
         out_banks = {}
         bias_terms = {}
+        grams = {}
         for step in range(-3, NT + LAG):
             multiplied = step + 1
             quantised = step + 2
@@ -354,6 +368,10 @@ def tile_hyplinear_kernel(tc, x, weight_words, weight_scales, bias, out):
                 spread = spread_bias()
             if 1 <= multiplied < NT:
                 stats_banks[multiplied] = product(multiplied, ps_stats)
+            if quantised in GRAM:
+                grams[quantised] = gram(quantised)
+            if multiplied in GRAM:
+                diagonal(multiplied, grams[multiplied])
             run_place(place)
             if written >= 0:
                 out_tile = out_pool.tile([P, N], F32, name="out_tile")
@@ -365,7 +383,7 @@ def tile_hyplinear_kernel(tc, x, weight_words, weight_scales, bias, out):
             if step == -2:
                 for half_n in range(2):
                     V.tensor_copy(out=bias_all[:, BANK * half_n : BANK * (half_n + 1)], in_=spread[half_n][:])
-            if 0 <= turned < VECTOR_COPIES:
+            if 0 <= turned < NT and turned < VECTOR_COPIES:
                 grouped[turned] = copy_tile(turned, transposed)
             if written >= 0:
                 write_half(written, out_banks[written][1], bias_terms[written], out_tile, 1)
@@ -384,7 +402,7 @@ def tile_hyplinear_kernel(tc, x, weight_words, weight_scales, bias, out):
             if 0 <= step < NT:
                 dot_with_bias(step, stats_banks[step][0], 0)
                 dot_with_bias(step, stats_banks[step][1], 1)
-            if VECTOR_COPIES <= turned < NT:
+            if 0 <= turned < NT and turned >= VECTOR_COPIES:
                 grouped[turned] = copy_tile(turned, transposed)
-            if 0 <= step + SQUARES_LEAD < NT:
+            if 0 <= step + SQUARES_LEAD < NT and step + SQUARES_LEAD not in GRAM:
                 x_norm(step + SQUARES_LEAD)

@@ -35,7 +35,7 @@ CHAIN_STEPS = 3
 LAG = max(GROUPS) + CHAIN_STEPS
 DRAIN = NT - LAG
 GRAM = range(4, 14, 2)
-SQUARES_LEAD = 3
+SQUARES_LEAD = 2
 VECTOR_COPIES = 6
 
 
@@ -48,8 +48,7 @@ def tile_hyplinear_kernel(tc, x, weight_words, weight_scales, bias, out):
         keep = ctx.enter_context(tc.tile_pool(name="keep", bufs=1))
         grouped_pool = ctx.enter_context(tc.tile_pool(name="grouped", bufs=3))
         unused = ctx.enter_context(tc.tile_pool(name="unused", bufs=6))
-        bias_term_pool = ctx.enter_context(tc.tile_pool(name="bias_term", bufs=3))
-        out_pool = ctx.enter_context(tc.tile_pool(name="out_tile", bufs=4))
+        out_pool = ctx.enter_context(tc.tile_pool(name="out_tile", bufs=8))
         ps_transposed = ctx.enter_context(tc.psum_pool(name="ps_transposed", bufs=1))
         ps_stats = ctx.enter_context(tc.psum_pool(name="ps_stats", bufs=4))
         ps_out = ctx.enter_context(tc.psum_pool(name="ps_out", bufs=3))
@@ -104,8 +103,8 @@ def tile_hyplinear_kernel(tc, x, weight_words, weight_scales, bias, out):
         sx = keep.tile([P, NT], F32)
         parts = keep.tile([P, 2, NT, 2], F32)
         sums = keep.tile([P, 2, NT], F32)
-        coef_mx = keep.tile([P, NT], F32)
-        coef_bias = keep.tile([P, NT], F32)
+        coefs = keep.tile([P, 2, NT], F32)
+        scaled_bias = keep.tile([P, N], F32)
         inv_xn = keep.tile([P, NT], F32)
         ratio = keep.tile([P, NT], F32)
 
@@ -136,7 +135,7 @@ def tile_hyplinear_kernel(tc, x, weight_words, weight_scales, bias, out):
             sb, sb_floor, inv_bias_norm, bias_norm = const("sb"), const("sb_floor"), const("inv_bias_norm"), const("bias_norm")
             e_squared, bias_power, inv_e, bias_tanh = const("e_squared"), const("bias_power"), const("inv_e"), const("bias_tanh")
             h, h_sq, y2, capped = const("h"), const("h_sq"), const("y2"), const("capped")
-            minus_4h, four_y2, eight_y2, one_plus_y2, clamp_slope = const("minus_4h"), const("four_y2"), const("eight_y2"), const("one_plus_y2"), const("clamp_slope")
+            two_h, minus_4h, four_y2, one_plus_y2, clamp_slope = const("two_h"), const("minus_4h"), const("four_y2"), const("one_plus_y2"), const("clamp_slope")
 
             def sum_of_squares():
                 squares = keep.tile([P, N], F32, name="bias_squares")
@@ -161,23 +160,25 @@ def tile_hyplinear_kernel(tc, x, weight_words, weight_scales, bias, out):
                 V.scalar_tensor_tensor(out=h[:], in0=bias_tanh[:], scalar=MAX_NORM, in1=inv_bias_norm[:], op0=AL.min, op1=AL.mult)
                 V.tensor_tensor(out=h_sq[:], in0=h[:], in1=h[:], op=AL.mult)
                 V.tensor_tensor(out=y2[:], in0=h_sq[:], in1=sb[:], op=AL.mult)
+                V.tensor_scalar_mul(out=two_h[:], in0=h[:], scalar1=2.0)
                 V.tensor_scalar_mul(out=minus_4h[:], in0=h[:], scalar1=-4.0)
+                nc.gpsimd.tensor_scalar(out=scaled_bias[:], in0=bias_all[:], scalar1=minus_4h[:], scalar2=0.0, op0=AL.mult, op1=AL.add)
 
             def constants():
                 V.tensor_scalar_mul(out=four_y2[:], in0=y2[:], scalar1=4.0)
-                V.tensor_scalar_mul(out=eight_y2[:], in0=y2[:], scalar1=8.0)
                 V.tensor_scalar_add(out=one_plus_y2[:], in0=y2[:], scalar1=1.0)
                 V.tensor_scalar(out=clamp_slope[:], in0=y2[:], scalar1=-4.0 / MAX_NORM2, scalar2=4.0 / MAX_NORM2, op0=AL.mult, op1=AL.add)
 
             for i, call in enumerate([sum_of_squares, norm, power, tanh, factors, constants]):
                 put(place + 2 * i, call)
-            return minus_4h, four_y2, eight_y2, one_plus_y2, clamp_slope
+            return two_h, four_y2, one_plus_y2, clamp_slope
 
         xn, u, one_minus_u, inv_one_minus_u = rows("xn"), rows("u"), rows("one_minus_u"), rows("inv_one_minus_u")
-        inv_mn, exponent, e_power, e_plus_1, q = rows("inv_mn"), rows("exponent"), rows("e_power"), rows("e_plus_1"), rows("q")
-        sm_over_xn, minus_beta, minus_res, den_part, two_xy = rows("sm_over_xn"), rows("minus_beta"), rows("minus_res"), rows("den_part"), rows("two_xy")
-        den, inv_den, minus_tau, shrink, alpha, unclamped = rows("den"), rows("inv_den"), rows("minus_tau"), rows("shrink"), rows("alpha"), rows("unclamped")
-        h_tau = rows("h_tau")
+        two_over_mn, exponent, e_power, e_plus_1, q = rows("two_over_mn"), rows("exponent"), rows("e_power"), rows("e_plus_1"), rows("q")
+        sm_over_xn, minus_res, den_part, minus_two_xy = rows("sm_over_xn"), rows("minus_res"), rows("den_part"), rows("minus_two_xy")
+        den, inv_den, shrink = rows("den"), rows("inv_den"), rows("shrink")
+        numerators = keep.tile([P, 2, NT], F32)
+        unclamped = keep.tile([P, 2, NT], F32)
 
         def x_scalars(place, g):
             def inverse():
@@ -205,13 +206,13 @@ def tile_hyplinear_kernel(tc, x, weight_words, weight_scales, bias, out):
         def row_scalars(place, g, count):
             def add_parts():
                 V.tensor_tensor(out=sums[:, :, g], in0=parts[:, :, g, 0], in1=parts[:, :, g, 1], op=AL.add)
-                for_scalar.append(lambda: nc.scalar.activation(out=inv_mn[:, g], in_=sums[:, 0, g], func=AF.Abs_reciprocal_sqrt, bias=MIN_SQ))
+                for_scalar.append(lambda: nc.scalar.activation(out=two_over_mn[:, g], in_=sums[:, 0, g], func=AF.Abs_reciprocal_sqrt, scale=0.25, bias=MIN_SQ / 4.0))
 
             def over_xn():
                 V.tensor_tensor(out=sm_over_xn[:, g], in0=sums[:, 0, g], in1=inv_xn[:, g], op=AL.mult)
 
             def power():
-                V.tensor_tensor(out=exponent[:, g], in0=sm_over_xn[:, g], in1=inv_mn[:, g], op=AL.mult)
+                V.scalar_tensor_tensor(out=exponent[:, g], in0=sm_over_xn[:, g], scalar=0.5, in1=two_over_mn[:, g], op0=AL.mult, op1=AL.mult)
                 nc.gpsimd.tensor_tensor(out=e_power[:, g], in0=ratio[:, g], in1=exponent[:, g], op=AL.pow)
 
             def clamp_power():
@@ -221,30 +222,28 @@ def tile_hyplinear_kernel(tc, x, weight_words, weight_scales, bias, out):
                 V.reciprocal(out=q[:, g], in_=e_plus_1[:, g])
 
             def from_q():
-                V.scalar_tensor_tensor(out=minus_beta[:, g], in0=q[:, g], scalar=1.0, in1=q[:, g], op0=AL.subtract, op1=AL.mult)
-                V.scalar_tensor_tensor(out=minus_res[:, g], in0=q[:, g], scalar=0.5, in1=inv_mn[:, g], op0=AL.subtract, op1=AL.mult)
-                V.tensor_scalar(out=den_part[:, g], in0=minus_beta[:, g], scalar1=four_y2[:], scalar2=one_plus_y2[:], op0=AL.mult, op1=AL.add)
-                V.scalar_tensor_tensor(out=two_xy[:, g], in0=sums[:, 1, g], scalar=minus_4h[:], in1=minus_res[:, g], op0=AL.mult, op1=AL.mult)
+                V.scalar_tensor_tensor(out=numerators[:, 1, g], in0=q[:, g], scalar=1.0, in1=q[:, g], op0=AL.subtract, op1=AL.mult)
+                V.scalar_tensor_tensor(out=minus_res[:, g], in0=q[:, g], scalar=0.5, in1=two_over_mn[:, g], op0=AL.subtract, op1=AL.mult)
+                V.tensor_scalar(out=den_part[:, g], in0=numerators[:, 1, g], scalar1=four_y2[:], scalar2=one_plus_y2[:], op0=AL.mult, op1=AL.add)
+                V.scalar_tensor_tensor(out=minus_two_xy[:, g], in0=sums[:, 1, g], scalar=two_h[:], in1=minus_res[:, g], op0=AL.mult, op1=AL.mult)
 
             def denominator():
-                V.tensor_tensor(out=den[:, g], in0=den_part[:, g], in1=two_xy[:, g], op=AL.add)
+                V.tensor_tensor(out=den[:, g], in0=den_part[:, g], in1=minus_two_xy[:, g], op=AL.subtract)
+                V.scalar_tensor_tensor(out=numerators[:, 0, g], in0=minus_two_xy[:, g], scalar=one_plus_y2[:], in1=minus_res[:, g], op0=AL.subtract, op1=AL.mult)
 
             def invert_denominator():
                 V.reciprocal(out=inv_den[:, g], in_=den[:, g])
 
-            def tau():
-                V.tensor_tensor(out=minus_tau[:, g], in0=minus_beta[:, g], in1=inv_den[:, g], op=AL.mult)
-                for_scalar.append(lambda: nc.scalar.activation(out=shrink[:, g], in_=minus_tau[:, g], func=AF.Abs_reciprocal_sqrt, scale=clamp_slope[:], bias=1.0 / MAX_NORM2))
+            def divide():
+                V.tensor_tensor(out=unclamped[:, :, g], in0=numerators[:, :, g], in1=inv_den[:, g].unsqueeze(1).to_broadcast([P, 2, count]), op=AL.mult)
+                for_scalar.append(lambda: nc.scalar.activation(out=shrink[:, g], in_=unclamped[:, 1, g], func=AF.Abs_reciprocal_sqrt, scale=clamp_slope[:], bias=1.0 / MAX_NORM2))
 
             def last():
-                V.tensor_scalar(out=alpha[:, g], in0=minus_tau[:, g], scalar1=eight_y2[:], scalar2=-2.0, op0=AL.mult, op1=AL.add)
-                V.tensor_scalar(out=h_tau[:, g], in0=minus_tau[:, g], scalar1=minus_4h[:], scalar2=1.0, op0=AL.mult, op1=AL.mult)
+                V.scalar_tensor_tensor(
+                    out=coefs[:, :, g], in0=shrink[:, g].unsqueeze(1).to_broadcast([P, 2, count]), scalar=1.0, in1=unclamped[:, :, g], op0=AL.min, op1=AL.mult
+                )
 
-                V.tensor_tensor(out=unclamped[:, g], in0=alpha[:, g], in1=minus_res[:, g], op=AL.mult)
-                V.scalar_tensor_tensor(out=coef_bias[:, g], in0=shrink[:, g], scalar=1.0, in1=h_tau[:, g], op0=AL.min, op1=AL.mult)
-                V.scalar_tensor_tensor(out=coef_mx[:, g], in0=shrink[:, g], scalar=1.0, in1=unclamped[:, g], op0=AL.min, op1=AL.mult)
-
-            calls = {1: add_parts, 2: over_xn, 3: power, 5: clamp_power, 6: invert_power, 7: from_q, 8: denominator, 9: invert_denominator, 10: tau, 11: last}
+            calls = {1: add_parts, 2: over_xn, 3: power, 5: clamp_power, 6: invert_power, 7: from_q, 8: denominator, 9: invert_denominator, 10: divide, 11: last}
 
             for offset, call in calls.items():
                 at = place + offset * min(LAG - count, CHAIN_STEPS + 3) // CHAIN_STEPS
@@ -328,20 +327,20 @@ def tile_hyplinear_kernel(tc, x, weight_words, weight_scales, bias, out):
             return spread
 
         def make_bias_term(t):
-            bias_term = bias_term_pool.tile([P, N], F32, name="bias_term")
+            out_tile = out_pool.tile([P, N], F32, name="out_tile")
             if t > DRAIN and t % 2 == 0:
-                nc.scalar.activation(out=bias_term[:], in_=bias_all[:], func=AF.Copy, scale=coef_bias[:, t : t + 1])
+                nc.scalar.activation(out=out_tile[:], in_=scaled_bias[:], func=AF.Copy, scale=coefs[:, 1, t : t + 1])
             else:
-                nc.gpsimd.tensor_scalar(out=bias_term[:], in0=bias_all[:], scalar1=coef_bias[:, t : t + 1], scalar2=0.0, op0=AL.mult, op1=AL.add)
-            return bias_term
+                nc.gpsimd.tensor_scalar(out=out_tile[:], in0=scaled_bias[:], scalar1=coefs[:, 1, t : t + 1], scalar2=0.0, op0=AL.mult, op1=AL.add)
+            return out_tile
 
-        def write_half(t, bank, bias_term, out_tile, half_n):
+        def write_half(t, bank, out_tile, half_n):
             cols = slice(BANK * half_n, BANK * (half_n + 1))
             V.scalar_tensor_tensor(
-                out=out_tile[:, cols], in0=bank[:], scalar=coef_mx[:, t : t + 1], in1=bias_term[:, cols], op0=AL.mult, op1=AL.add
+                out=out_tile[:, cols], in0=bank[:], scalar=coefs[:, 0, t : t + 1], in1=out_tile[:, cols], op0=AL.mult, op1=AL.add
             )
 
-        minus_4h, four_y2, eight_y2, one_plus_y2, clamp_slope = bias_numbers(4 * SLOTS)
+        two_h, four_y2, one_plus_y2, clamp_slope = bias_numbers(4 * SLOTS)
         first = 0
         for count in GROUPS:
             last_tile = first + count - 1
@@ -374,8 +373,7 @@ def tile_hyplinear_kernel(tc, x, weight_words, weight_scales, bias, out):
                 diagonal(multiplied, grams[multiplied])
             run_place(place)
             if written >= 0:
-                out_tile = out_pool.tile([P, N], F32, name="out_tile")
-                write_half(written, out_banks[written][0], bias_terms[written], out_tile, 0)
+                write_half(written, out_banks[written][0], bias_terms[written], 0)
             run_place(place + 1)
             if 0 <= quantised < NT:
                 quantise_tile(quantised, grouped[quantised])
@@ -386,8 +384,8 @@ def tile_hyplinear_kernel(tc, x, weight_words, weight_scales, bias, out):
             if 0 <= turned < NT and turned < VECTOR_COPIES:
                 grouped[turned] = copy_tile(turned, transposed)
             if written >= 0:
-                write_half(written, out_banks[written][1], bias_terms[written], out_tile, 1)
-                nc.sync.dma_start(out=out_rows[:, written, :], in_=out_tile[:])
+                write_half(written, out_banks[written][1], bias_terms[written], 1)
+                nc.sync.dma_start(out=out_rows[:, written, :], in_=bias_terms[written][:])
             if 0 <= step < NT:
                 sum_of_squares(step, stats_banks[step][0], 0)
             run_for_scalar()

@@ -31,7 +31,7 @@ MAX_E = 2.0 / (1.0 - MAX_NORM) - 1.0
 X_LOADS = [1, 1, 1, 1, 2, 2, 4, 4, 4, 4, 4, 4]
 GROUPS = [8, 8, 8, 4, 4]
 SLOTS = 4
-CHAIN_STEPS = 3
+CHAIN_STEPS = 4
 LAG = max(GROUPS) + CHAIN_STEPS
 DRAIN = NT - LAG
 GRAM = range(4, 14, 2)
@@ -243,7 +243,7 @@ def tile_hyplinear_kernel(tc, x, weight_words, weight_scales, bias, out):
                     out=coefs[:, :, g], in0=shrink[:, g].unsqueeze(1).to_broadcast([P, 2, count]), scalar=1.0, in1=unclamped[:, :, g], op0=AL.min, op1=AL.mult
                 )
 
-            calls = {1: add_parts, 2: over_xn, 3: power, 5: clamp_power, 6: invert_power, 7: from_q, 8: denominator, 9: invert_denominator, 10: divide, 11: last}
+            calls = {1: add_parts, 2: over_xn, 3: power, 7: clamp_power, 8: invert_power, 9: from_q, 10: denominator, 11: invert_denominator, 13: divide, 15: last}
 
             for offset, call in calls.items():
                 at = place + offset * min(LAG - count, CHAIN_STEPS + 3) // CHAIN_STEPS
@@ -328,7 +328,7 @@ def tile_hyplinear_kernel(tc, x, weight_words, weight_scales, bias, out):
 
         def make_bias_term(t):
             out_tile = out_pool.tile([P, N], F32, name="out_tile")
-            if t > DRAIN and t % 2 == 0:
+            if t > DRAIN:
                 nc.scalar.activation(out=out_tile[:], in_=scaled_bias[:], func=AF.Copy, scale=coefs[:, 1, t : t + 1])
             else:
                 nc.gpsimd.tensor_scalar(out=out_tile[:], in0=scaled_bias[:], scalar1=coefs[:, 1, t : t + 1], scalar2=0.0, op0=AL.mult, op1=AL.add)
@@ -374,18 +374,23 @@ def tile_hyplinear_kernel(tc, x, weight_words, weight_scales, bias, out):
             run_place(place)
             if written >= 0:
                 write_half(written, out_banks[written][0], bias_terms[written], 0)
+            if written == NT - 1:
+                nc.sync.dma_start(out=out_rows[:, written, :BANK], in_=bias_terms[written][:, :BANK])
             run_place(place + 1)
             if 0 <= quantised < NT:
                 quantise_tile(quantised, grouped[quantised])
             run_place(place + 2)
             if step == -2:
                 for half_n in range(2):
-                    V.tensor_copy(out=bias_all[:, BANK * half_n : BANK * (half_n + 1)], in_=spread[half_n][:])
+                    nc.scalar.copy(out=bias_all[:, BANK * half_n : BANK * (half_n + 1)], in_=spread[half_n][:])
             if 0 <= turned < NT and turned < VECTOR_COPIES:
                 grouped[turned] = copy_tile(turned, transposed)
             if written >= 0:
                 write_half(written, out_banks[written][1], bias_terms[written], 1)
-                nc.sync.dma_start(out=out_rows[:, written, :], in_=bias_terms[written][:])
+                if written < NT - 1:
+                    nc.sync.dma_start(out=out_rows[:, written, :], in_=bias_terms[written][:])
+                else:
+                    nc.sync.dma_start(out=out_rows[:, written, BANK:], in_=bias_terms[written][:, BANK:])
             if 0 <= step < NT:
                 sum_of_squares(step, stats_banks[step][0], 0)
             run_for_scalar()

import math
from contextlib import ExitStack

import concourse.mybir as mybir
from concourse.masks import make_identity

F32 = mybir.dt.float32
BF16 = mybir.dt.bfloat16
U8 = mybir.dt.uint8
U32 = mybir.dt.uint32
I32 = mybir.dt.int32
FP8X4 = mybir.dt.float8_e4m3fn_x4
FP4X4 = mybir.dt.float4_e2m1fn_x4
AL = mybir.AluOpType
AF = mybir.ActivationFunctionType

P = 128
ROWS = 4096
K = 1024
N = 1024
NT = ROWS // P
PASSES = K // 512
BANK = 512
FLOPS = 2 * ROWS * K * N

MAX_NORM = 0.996
MAX_NORM2 = MAX_NORM * MAX_NORM
MIN_SQ = 1e-15
MAX_E = 2.0 / (1.0 - MAX_NORM) - 1.0

X_LOADS = [1, 1, 1, 1, 2, 2, 4, 4, 4, 4, 4, 4]
GROUPS = [8, 8, 8, 4, 4]
SLOTS = 4
CHAIN_STEPS = 4
LAG = max(GROUPS) + CHAIN_STEPS
DRAIN = NT - LAG
GRAM = range(4, 14, 2)
SQUARES_LEAD = 2
VECTOR_COPIES = 6


def tile_hyplinear_kernel(tc, x, weight_words, weight_scales, bias, out):
    nc = tc.nc
    x_rows = x.rearrange("(p t) k -> p t k", t=NT)
    out_rows = out.rearrange("(p t) n -> p t n", t=NT)

    with ExitStack() as ctx:
        keep = ctx.enter_context(tc.tile_pool(name="keep", bufs=1))
        grouped_pool = ctx.enter_context(tc.tile_pool(name="grouped", bufs=3))
        unused = ctx.enter_context(tc.tile_pool(name="unused", bufs=6))
        out_pool = ctx.enter_context(tc.tile_pool(name="out_tile", bufs=8))
        ps_transposed = ctx.enter_context(tc.psum_pool(name="ps_transposed", bufs=1))
        ps_stats = ctx.enter_context(tc.psum_pool(name="ps_stats", bufs=4))
        ps_out = ctx.enter_context(tc.psum_pool(name="ps_out", bufs=3))
        ctx.enter_context(tc.manual_schedule())
        V = nc.vector

        warm = keep.tile([P, 1], F32)
        V.memset(warm[:], 1.0)
        nc.scalar.activation(out=warm[:], in_=warm[:], func=AF.Abs_reciprocal_sqrt)
        identity = keep.tile([P, P], F32)
        make_identity(nc, identity[:])
        bias_row = keep.tile([P, N], BF16)
        V.memset(bias_row[:], 0.0)
        ones = keep.tile([P, P], BF16)
        V.memset(ones[:], 1.0)
        w_scales = keep.tile([P, PASSES, N], U8, align_bytes=64)
        V.memset(w_scales[:].bitcast(I32), 0)
        zero = keep.tile([P, 1], F32)
        V.memset(zero[:], 0.0)
        half = keep.tile([P, 1], F32)
        V.memset(half[:], 0.5)

        x_tiles = []
        x_loads = []
        for i, count in enumerate(X_LOADS):
            loaded = keep.tile([P, count, K], BF16, name="x%d" % i)
            x_loads.append((loaded, len(x_tiles), count))
            for j in range(count):
                x_tiles.append(loaded[:, j, :])

        def load_x(i):
            loaded, first, count = x_loads[i]
            nc.sync.dma_start(out=loaded[:], in_=x_rows[:, first : first + count, :])

        load_x(0)
        load_x(1)
        nc.sync.dma_start(out=bias_row[0:1, :], in_=bias.rearrange("(o n) -> o n", o=1))
        scales32 = weight_scales.bitcast(I32)
        for quadrant in range(4):
            nc.sync.dma_start(
                out=w_scales[32 * quadrant : 32 * quadrant + 4].bitcast(I32),
                in_=scales32[:, 4 * quadrant : 4 * quadrant + 4, :].rearrange("g r n -> r g n"),
            )
        w_codes = keep.tile([P, PASSES, 2 * N], U8, align_bytes=64)
        nc.sync.dma_start(out=w_codes[:].bitcast(I32), in_=weight_words.bitcast(I32).rearrange("g p n -> p g n"))
        for i in range(2, len(X_LOADS)):
            load_x(i)

        bias_all = keep.tile([P, N], BF16)
        x_codes = keep.tile([P, NT, PASSES * P], U32, align_bytes=64)
        x_scales = keep.tile([P, NT, PASSES * P], U8, align_bytes=64)
        sx = keep.tile([P, NT], F32)
        parts = keep.tile([P, 2, NT, 2], F32)
        sums = keep.tile([P, 2, NT], F32)
        coefs = keep.tile([P, 2, NT], F32)
        scaled_bias = keep.tile([P, N], F32)
        inv_xn = keep.tile([P, NT], F32)
        ratio = keep.tile([P, NT], F32)

        known = {}
        waiting = {}

        def put(place, call):
            waiting.setdefault(place, []).append(call)

        def run_place(place):
            for call in waiting.get(place, []):
                call()

        for_scalar = []

        def run_for_scalar():
            for call in for_scalar:
                call()
            for_scalar.clear()

        def const(name):
            return keep.tile([P, 1], F32, name=name)

        def rows(name):
            return keep.tile([P, NT], F32, name=name)

        def bias_numbers(place):
            sb, sb_floor, inv_bias_norm, bias_norm = const("sb"), const("sb_floor"), const("inv_bias_norm"), const("bias_norm")
            e_squared, bias_power, inv_e, bias_tanh = const("e_squared"), const("bias_power"), const("inv_e"), const("bias_tanh")
            h, h_sq, y2, capped = const("h"), const("h_sq"), const("y2"), const("capped")
            two_h, minus_4h, four_y2, one_plus_y2, clamp_slope = const("two_h"), const("minus_4h"), const("four_y2"), const("one_plus_y2"), const("clamp_slope")

            def sum_of_squares():
                squares = keep.tile([P, N], F32, name="bias_squares")
                V.scalar_tensor_tensor(out=squares[:], in0=bias_all[:], scalar=1.0, in1=bias_all[:], op0=AL.mult, op1=AL.mult, accum_out=sb[:])
                V.tensor_scalar_add(out=e_squared[:], in0=zero[:], scalar1=math.exp(2.0))

            def norm():
                V.tensor_scalar_max(out=sb_floor[:], in0=sb[:], scalar1=MIN_SQ)
                nc.gpsimd.tensor_tensor(out=bias_norm[:], in0=sb_floor[:], in1=half[:], op=AL.pow)

            def power():
                V.reciprocal(out=inv_bias_norm[:], in_=bias_norm[:])
                V.tensor_scalar_min(out=capped[:], in0=bias_norm[:], scalar1=30.0)
                nc.gpsimd.tensor_tensor(out=bias_power[:], in0=e_squared[:], in1=capped[:], op=AL.pow)

            def tanh():
                V.tensor_scalar_add(out=bias_power[:], in0=bias_power[:], scalar1=1.0)
                V.reciprocal(out=inv_e[:], in_=bias_power[:])
                V.tensor_scalar(out=bias_tanh[:], in0=inv_e[:], scalar1=-2.0, scalar2=1.0, op0=AL.mult, op1=AL.add)

            def factors():
                V.scalar_tensor_tensor(out=h[:], in0=bias_tanh[:], scalar=MAX_NORM, in1=inv_bias_norm[:], op0=AL.min, op1=AL.mult)
                V.tensor_tensor(out=h_sq[:], in0=h[:], in1=h[:], op=AL.mult)
                V.tensor_tensor(out=y2[:], in0=h_sq[:], in1=sb[:], op=AL.mult)
                V.tensor_scalar_mul(out=two_h[:], in0=h[:], scalar1=2.0)
                V.tensor_scalar_mul(out=minus_4h[:], in0=h[:], scalar1=-4.0)
                nc.gpsimd.tensor_scalar(out=scaled_bias[:], in0=bias_all[:], scalar1=minus_4h[:], scalar2=0.0, op0=AL.mult, op1=AL.add)

            def constants():
                V.tensor_scalar_mul(out=four_y2[:], in0=y2[:], scalar1=4.0)
                V.tensor_scalar_add(out=one_plus_y2[:], in0=y2[:], scalar1=1.0)
                V.tensor_scalar(out=clamp_slope[:], in0=y2[:], scalar1=-4.0 / MAX_NORM2, scalar2=4.0 / MAX_NORM2, op0=AL.mult, op1=AL.add)

            for i, call in enumerate([sum_of_squares, norm, power, tanh, factors, constants]):
                put(place + 2 * i, call)
            return two_h, four_y2, one_plus_y2, clamp_slope

        xn, u, one_minus_u, inv_one_minus_u = rows("xn"), rows("u"), rows("one_minus_u"), rows("inv_one_minus_u")
        two_over_mn, exponent, e_power, e_plus_1, q = rows("two_over_mn"), rows("exponent"), rows("e_power"), rows("e_plus_1"), rows("q")
        sm_over_xn, minus_res, den_part, minus_two_xy = rows("sm_over_xn"), rows("minus_res"), rows("den_part"), rows("minus_two_xy")
        den, inv_den, shrink = rows("den"), rows("inv_den"), rows("shrink")
        numerators = keep.tile([P, 2, NT], F32)
        unclamped = keep.tile([P, 2, NT], F32)

        def x_scalars(place, g):
            def inverse():
                for_scalar.append(lambda: nc.scalar.activation(out=inv_xn[:, g], in_=sx[:, g], func=AF.Abs_reciprocal_sqrt, bias=MIN_SQ))

            def norm():
                V.tensor_tensor(out=xn[:, g], in0=sx[:, g], in1=inv_xn[:, g], op=AL.mult)

            def clamp():
                V.tensor_scalar_min(out=u[:, g], in0=xn[:, g], scalar1=1.0 - 1e-5)

            def difference():
                V.tensor_scalar(out=one_minus_u[:, g], in0=u[:, g], scalar1=-1.0, scalar2=1.0, op0=AL.mult, op1=AL.add)

            def invert():
                V.reciprocal(out=inv_one_minus_u[:, g], in_=one_minus_u[:, g])

            def quotient():
                V.scalar_tensor_tensor(out=ratio[:, g], in0=u[:, g], scalar=1.0, in1=inv_one_minus_u[:, g], op0=AL.add, op1=AL.mult)

            put(place, inverse)
            for i, call in enumerate([norm, clamp, difference, invert, quotient]):
                put(place + 3 + i, call)

        def row_scalars(place, g, count):
            def add_parts():
                V.tensor_tensor(out=sums[:, :, g], in0=parts[:, :, g, 0], in1=parts[:, :, g, 1], op=AL.add)
                for_scalar.append(lambda: nc.scalar.activation(out=two_over_mn[:, g], in_=sums[:, 0, g], func=AF.Abs_reciprocal_sqrt, scale=0.25, bias=MIN_SQ / 4.0))

            def over_xn():
                V.tensor_tensor(out=sm_over_xn[:, g], in0=sums[:, 0, g], in1=inv_xn[:, g], op=AL.mult)

            def power():
                V.scalar_tensor_tensor(out=exponent[:, g], in0=sm_over_xn[:, g], scalar=0.5, in1=two_over_mn[:, g], op0=AL.mult, op1=AL.mult)
                nc.gpsimd.tensor_tensor(out=e_power[:, g], in0=ratio[:, g], in1=exponent[:, g], op=AL.pow)

            def clamp_power():
                V.tensor_scalar(out=e_plus_1[:, g], in0=e_power[:, g], scalar1=MAX_E, scalar2=1.0, op0=AL.min, op1=AL.add)

            def invert_power():
                V.reciprocal(out=q[:, g], in_=e_plus_1[:, g])

            def from_q():
                V.scalar_tensor_tensor(out=numerators[:, 1, g], in0=q[:, g], scalar=1.0, in1=q[:, g], op0=AL.subtract, op1=AL.mult)
                V.scalar_tensor_tensor(out=minus_res[:, g], in0=q[:, g], scalar=0.5, in1=two_over_mn[:, g], op0=AL.subtract, op1=AL.mult)
                V.tensor_scalar(out=den_part[:, g], in0=numerators[:, 1, g], scalar1=four_y2[:], scalar2=one_plus_y2[:], op0=AL.mult, op1=AL.add)
                V.scalar_tensor_tensor(out=minus_two_xy[:, g], in0=sums[:, 1, g], scalar=two_h[:], in1=minus_res[:, g], op0=AL.mult, op1=AL.mult)

            def denominator():
                V.tensor_tensor(out=den[:, g], in0=den_part[:, g], in1=minus_two_xy[:, g], op=AL.subtract)
                V.scalar_tensor_tensor(out=numerators[:, 0, g], in0=minus_two_xy[:, g], scalar=one_plus_y2[:], in1=minus_res[:, g], op0=AL.subtract, op1=AL.mult)

            def invert_denominator():
                V.reciprocal(out=inv_den[:, g], in_=den[:, g])

            def divide():
                V.tensor_tensor(out=unclamped[:, :, g], in0=numerators[:, :, g], in1=inv_den[:, g].unsqueeze(1).to_broadcast([P, 2, count]), op=AL.mult)
                for_scalar.append(lambda: nc.scalar.activation(out=shrink[:, g], in_=unclamped[:, 1, g], func=AF.Abs_reciprocal_sqrt, scale=clamp_slope[:], bias=1.0 / MAX_NORM2))

            def last():
                V.scalar_tensor_tensor(
                    out=coefs[:, :, g], in0=shrink[:, g].unsqueeze(1).to_broadcast([P, 2, count]), scalar=1.0, in1=unclamped[:, :, g], op0=AL.min, op1=AL.mult
                )

            calls = {1: add_parts, 2: over_xn, 3: power, 7: clamp_power, 8: invert_power, 9: from_q, 10: denominator, 11: invert_denominator, 13: divide, 15: last}

            for offset, call in calls.items():
                at = place + offset * min(LAG - count, CHAIN_STEPS + 3) // CHAIN_STEPS
                if call == last:
                    at = (at // SLOTS + 1) * SLOTS - 1
                put(at, call)
            for t in range(g.start, g.stop):
                known[t] = at

        def transpose_tile(t):
            words = x_tiles[t].bitcast(F32)
            transposed = ps_transposed.tile([P, 2 * PASSES, P], F32, name="transposed")
            for g in range(PASSES):
                for u in range(2):
                    nc.tensor.transpose(transposed[:, 2 * g + u, :], words[:, 256 * g + u : 256 * (g + 1) : 2], identity[:])
            return transposed

        def copy_tile(t, transposed):
            grouped = grouped_pool.tile([P, K], BF16, name="grouped", align_bytes=64)
            dst = grouped[:].bitcast(F32).rearrange("p (g r u) -> p g r u", g=PASSES, u=2)
            src = transposed[:].rearrange("p (g u) r -> p g r u", g=PASSES)
            if t < VECTOR_COPIES:
                V.tensor_copy(out=dst, in_=src)
            else:
                nc.scalar.copy(out=dst, in_=src)
            return grouped

        def quantise_tile(t, grouped):
            V.quantize_mx(out=x_codes[:, t, :].bitcast(FP8X4), scales=x_scales[:, t, :], in_=grouped[:])

        def gram(t):
            columns = grouped[t][:].rearrange("p (g r e) -> p g e r", g=PASSES, e=4)
            bank = ps_out.tile([P, P], F32, name="mx")
            for g in range(PASSES):
                for e in range(4):
                    nc.tensor.matmul(out=bank[:], lhsT=columns[:, g, e, :], rhs=columns[:, g, e, :], start=(g + e == 0), stop=(g == PASSES - 1 and e == 3))
            return bank

        def diagonal(t, bank):
            picked = unused.tile([P, P], F32, name="picked")
            V.scalar_tensor_tensor(out=picked[:], in0=bank[:], scalar=1.0, in1=identity[:], op0=AL.mult, op1=AL.mult, accum_out=sx[:, t : t + 1])

        def x_norm(t):
            squares = unused.tile([P, K], BF16, name="x_squares")
            nc.scalar.activation(out=squares[:], in_=x_tiles[t], func=AF.Square, accum_out=sx[:, t : t + 1])

        def product(t, pool):
            banks = []
            for half_n in range(2):
                bank = pool.tile([P, BANK], F32, name="mx")
                banks.append(bank)
                for g in range(PASSES):
                    nc.tensor.matmul_mx(
                        out=bank[:],
                        lhsT=x_codes[:, t, P * g : P * (g + 1)].bitcast(FP8X4),
                        lhsT_scale=x_scales[:, t, P * g : P * (g + 1)],
                        rhs=w_codes[:, g, 2 * BANK * half_n : 2 * BANK * (half_n + 1)].bitcast(FP4X4),
                        rhs_scale=w_scales[:, g, BANK * half_n : BANK * (half_n + 1)],
                        start=(g == 0),
                        stop=(g == PASSES - 1),
                    )
            return banks

        def sum_of_squares(t, bank, half_n):
            squares = unused.tile([P, BANK], BF16, name="mx_squares")
            nc.scalar.activation(out=squares[:], in_=bank[:], func=AF.Square, accum_out=parts[:, 0, t, half_n : half_n + 1])

        def dot_with_bias(t, bank, half_n):
            products = unused.tile([P, BANK], F32, name="products")
            V.scalar_tensor_tensor(
                out=products[:], in0=bank[:], scalar=1.0, in1=bias_all[:, BANK * half_n : BANK * (half_n + 1)],
                op0=AL.mult, op1=AL.mult, accum_out=parts[:, 1, t, half_n : half_n + 1],
            )

        def spread_bias():
            spread = []
            for half_n in range(2):
                bank = ps_out.tile([P, BANK], F32, name="mx")
                nc.tensor.matmul(out=bank[:], lhsT=ones[:], rhs=bias_row[:, BANK * half_n : BANK * (half_n + 1)], start=True, stop=True)
                spread.append(bank)
            return spread

        def make_bias_term(t):
            out_tile = out_pool.tile([P, N], F32, name="out_tile")
            if t > DRAIN:
                nc.scalar.activation(out=out_tile[:], in_=scaled_bias[:], func=AF.Copy, scale=coefs[:, 1, t : t + 1])
            else:
                nc.gpsimd.tensor_scalar(out=out_tile[:], in0=scaled_bias[:], scalar1=coefs[:, 1, t : t + 1], scalar2=0.0, op0=AL.mult, op1=AL.add)
            return out_tile

        def write_half(t, bank, out_tile, half_n):
            cols = slice(BANK * half_n, BANK * (half_n + 1))
            V.scalar_tensor_tensor(
                out=out_tile[:, cols], in0=bank[:], scalar=coefs[:, 0, t : t + 1], in1=out_tile[:, cols], op0=AL.mult, op1=AL.add
            )

        two_h, four_y2, one_plus_y2, clamp_slope = bias_numbers(4 * SLOTS)
        first = 0
        for count in GROUPS:
            last_tile = first + count - 1
            x_scalars(SLOTS * (last_tile + 1 - SQUARES_LEAD) + 1, slice(first, first + count))
            row_scalars(SLOTS * (last_tile + 1), slice(first, first + count), count)
            first += count

        grouped = {}
        stats_banks = {}
        out_banks = {}
        bias_terms = {}
        grams = {}
        for step in range(-3, NT + LAG):
            multiplied = step + 1
            quantised = step + 2
            turned = step + 3
            written = step - LAG
            place = SLOTS * step
            if step == -1:
                stats_banks[multiplied] = product(multiplied, ps_stats)
            if 0 <= turned < NT:
                transposed = transpose_tile(turned)
            if step == -3:
                spread = spread_bias()
            if 1 <= multiplied < NT:
                stats_banks[multiplied] = product(multiplied, ps_stats)
            if quantised in GRAM:
                grams[quantised] = gram(quantised)
            if multiplied in GRAM:
                diagonal(multiplied, grams[multiplied])
            run_place(place)
            if written >= 0:
                write_half(written, out_banks[written][0], bias_terms[written], 0)
            if written == NT - 1:
                nc.sync.dma_start(out=out_rows[:, written, :BANK], in_=bias_terms[written][:, :BANK])
            run_place(place + 1)
            if 0 <= quantised < NT:
                quantise_tile(quantised, grouped[quantised])
            run_place(place + 2)
            if step == -2:
                for half_n in range(2):
                    nc.scalar.copy(out=bias_all[:, BANK * half_n : BANK * (half_n + 1)], in_=spread[half_n][:])
            if 0 <= turned < NT and turned < VECTOR_COPIES:
                grouped[turned] = copy_tile(turned, transposed)
            if written >= 0:
                write_half(written, out_banks[written][1], bias_terms[written], 1)
                if written < NT - 1:
                    nc.sync.dma_start(out=out_rows[:, written, :], in_=bias_terms[written][:])
                else:
                    nc.sync.dma_start(out=out_rows[:, written, BANK:], in_=bias_terms[written][:, BANK:])
            if 0 <= step < NT:
                sum_of_squares(step, stats_banks[step][0], 0)
            run_for_scalar()
            if 0 <= step < NT:
                sum_of_squares(step, stats_banks[step][1], 1)
            run_place(place + 3)
            for t in range(max(written + 1, 0), min(written + 3, NT)):
                if t not in bias_terms and known[t] <= place + 3:
                    bias_terms[t] = make_bias_term(t)
            if 0 <= written + 1 < NT:
                out_banks[written + 1] = product(written + 1, ps_out)
            if 0 <= step < NT:
                dot_with_bias(step, stats_banks[step][0], 0)
                dot_with_bias(step, stats_banks[step][1], 1)
            if 0 <= turned < NT and turned >= VECTOR_COPIES:
                grouped[turned] = copy_tile(turned, transposed)
            if 0 <= step + SQUARES_LEAD < NT and step + SQUARES_LEAD not in GRAM:
                x_norm(step + SQUARES_LEAD)
